import numpy as np
import ml_dtypes


def mxq(x, axis, fmt="e4m3"):
    dtype, down = {"e4m3": (ml_dtypes.float8_e4m3fn, 7), "e5m2": (ml_dtypes.float8_e5m2, 14)}[fmt]
    v = np.moveaxis(np.asarray(x, np.float32).astype(ml_dtypes.bfloat16).astype(np.float64), axis, -1)
    blocks = v.reshape(v.shape[:-1] + (-1, 32))
    amax = np.abs(blocks).max(-1, keepdims=True)
    byte = np.maximum(np.where(amax > 0, np.frexp(amax)[1] - 1 + 127, 0) - down, 1)
    scale = np.exp2(byte - 127.0)
    codes = (blocks / scale).astype(np.float32).astype(dtype).astype(np.float64)
    return np.moveaxis((codes * scale).reshape(v.shape), -1, axis)


WIDE = False


def mx_kscale(k):
    if not WIDE:
        return np.ones(k)
    levels = np.array([10, -10, 5, -5, 0])
    a = np.random.permutation(np.resize(levels, k // 512 * 4)).reshape(k // 512, 4)
    idx = np.arange(k)
    return np.exp2(a[idx // 512, idx % 128 // 32])


BF16 = ml_dtypes.bfloat16


def bf(x):
    return np.asarray(x, np.float32).astype(BF16)


def f64(x):
    return np.asarray(x).astype(np.float64)


E2M1 = np.array([0.0, 0.5, 1.0, 1.5, 2.0, 3.0, 4.0, 6.0, -0.0, -0.5, -1.0, -1.5, -2.0, -3.0, -4.0, -6.0])


def pack_weight(w, fmt):
    k, n = w.shape
    w = f64(bf(w)).reshape(k // 32, 32, n)
    amax = np.abs(w).max(1)
    if fmt == "e4m3":
        byte = np.frexp(amax)[1] - 1 + 127 - 7
    else:
        mant, ex = np.frexp(amax / 6.0)
        byte = np.where(mant > 0.5, ex, ex - 1) + 127
    byte = np.clip(np.where(amax > 0, byte, 1), 1, 254)
    scaled = (w * np.exp2(127.0 - byte)[:, None, :]).reshape(k, n).astype(np.float32)
    by_word = np.ascontiguousarray(scaled.reshape(k // 512, 128, 4, n).transpose(0, 1, 3, 2))
    if fmt == "e4m3":
        words = by_word.astype(ml_dtypes.float8_e4m3fn).view(np.uint8)
    else:
        c = by_word.astype(ml_dtypes.float4_e2m1fn).view(np.uint8) & 0xF
        words = c[..., 0::2] | (c[..., 1::2] << 4)
    return np.ascontiguousarray(words), np.ascontiguousarray(byte.astype(np.uint8).reshape(k // 512, 16, n))


def unpack_weight(words, scales, fmt):
    g, p, n, _ = words.shape
    if fmt == "e4m3":
        vals = np.ascontiguousarray(words).view(ml_dtypes.float8_e4m3fn).astype(np.float64)
    else:
        nib = np.empty((g, p, n, 4), np.uint8)
        nib[..., 0::2] = words & 0xF
        nib[..., 1::2] = words >> 4
        vals = E2M1[nib]
    vals = vals * np.repeat(np.exp2(scales.astype(np.float64) - 127.0), 8, axis=1)[..., None]
    return vals.transpose(0, 1, 3, 2).reshape(g * 512, n)

def pack4(w):
    words, scales = pack_weight(w, "e2m1")
    return words.reshape(words.shape[0], 128, -1), scales


def unpack4(words, scales):
    return unpack_weight(words.reshape(words.shape[0], 128, -1, 2), scales, "e2m1")


B, S, D, NH, NKV, HD = 2, 64, 512, 16, 4, 128
EPS = 1e-6
QS = NH * HD
KS = NKV * HD
E = QS + KS + KS
HP = HD // 2


def rmsnorm(v, w):
    ms = np.mean(np.square(v), axis=-1, keepdims=True)
    return v * (1.0 / np.sqrt(ms + EPS)) * w


def apply_rotary_emb(v, fc):
    vs = v.reshape(*v.shape[:-1], HP, 2)
    f = fc[None, :, None, :, :]
    vr, vi = vs[..., 0], vs[..., 1]
    fr, fi = f[..., 0], f[..., 1]
    return np.stack([vr * fr - vi * fi, vi * fr + vr * fi], axis=-1).reshape(v.shape)


def setup_inputs():
    s = mx_kscale(D)
    x = bf(np.random.standard_normal((B, S, D)) * s)
    freqs_cis = bf(np.random.standard_normal((S, HP, 2)))
    wqkv = np.random.standard_normal((E, D)) / np.sqrt(D) / s[None, :]
    words, scales = pack4(np.ascontiguousarray(wqkv.T))
    q_norm_w = bf(1.0 + 0.1 * np.random.standard_normal(HD))
    k_norm_w = bf(1.0 + 0.1 * np.random.standard_normal(HD))
    return {"x": x,
            "freqs_cis": freqs_cis,
            "wqkv_words": words,
            "wqkv_scales": scales,
            "q_norm_w": q_norm_w,
            "k_norm_w": k_norm_w}


def reference(x, freqs_cis, wqkv_words, wqkv_scales, q_norm_w, k_norm_w):
    fc = f64(freqs_cis)
    qkv = mxq(f64(x), 2, "e4m3") @ unpack4(wqkv_words, wqkv_scales)
    q = qkv[..., :QS].reshape(B, S, NH, HD)
    k = qkv[..., QS:QS + KS].reshape(B, S, NKV, HD)
    v = qkv[..., QS + KS:].reshape(B, S, NKV, HD)
    q = rmsnorm(q, f64(q_norm_w))
    k = rmsnorm(k, f64(k_norm_w))
    q_rot = apply_rotary_emb(q, fc)
    k_rot = apply_rotary_emb(k, fc)
    return q_rot, k_rot, v

@@ -1,0 +1,190 @@
+from contextlib import ExitStack
+
+import concourse.mybir as mybir
+from concourse.masks import make_identity
+
+F32 = mybir.dt.float32
+BF16 = mybir.dt.bfloat16
+I32 = mybir.dt.int32
+U8 = mybir.dt.uint8
+U32 = mybir.dt.uint32
+FP8X4 = mybir.dt.float8_e4m3fn_x4
+FP4X4 = mybir.dt.float4_e2m1fn_x4
+ACT = mybir.ActivationFunctionType
+ALU = mybir.AluOpType
+
+P = 128
+SEQ = 64
+K = 512
+HEAD = 128
+PAIRS = HEAD // 2
+BANK = 512
+HEADS_PER_BANK = BANK // HEAD
+Q_BANKS = 4
+K_BANK = 4
+V_BANK = 5
+NORMED_BANKS = Q_BANKS + 1
+N_BANKS = 6
+COLS = N_BANKS * BANK
+EPS = 1e-6
+
+FLOPS = 2 * P * K * COLS
+
+
+def tile_attention_pa_s_kernel(
+    tc, x, freqs_cis, wqkv_words, wqkv_scales, q_norm_w, k_norm_w, out_0, out_1, out_2
+):
+    nc = tc.nc
+    q_out = out_0.rearrange("b s h d -> (b s) (h d)")
+    k_out = out_1.rearrange("b s h d -> (b s) (h d)")
+    v_out = out_2.rearrange("b s h d -> (b s) (h d)")
+
+    with ExitStack() as ctx:
+        sbuf = ctx.enter_context(tc.tile_pool(name="sbuf", bufs=1))
+        psum = ctx.enter_context(tc.psum_pool(name="psum", bufs=1))
+        ctx.enter_context(tc.manual_schedule())
+
+        x_sb = sbuf.tile([P, K], BF16)
+        nc.sync.dma_start(out=x_sb[:], in_=x.flatten_outer_dims())
+
+        fc_sb = sbuf.tile([P, HEAD], BF16)
+        fc_rows = freqs_cis.rearrange("s j e -> s (j e)")
+        nc.scalar.dma_start(
+            out=fc_sb[:], in_=fc_rows.unsqueeze(0).to_broadcast([P // SEQ, SEQ, HEAD])
+        )
+        q_gain = sbuf.tile([P, HEAD], BF16)
+        nc.scalar.dma_start(out=q_gain[:], in_=q_norm_w.partition_broadcast(P))
+
+        eps = sbuf.tile([P, 1], F32)
+        nc.vector.memset(eps[:], EPS)
+        w_scales = sbuf.tile([P, COLS], U8, align_bytes=64)
+        nc.vector.memset(w_scales[:].bitcast(I32), 0)
+        for r in range(4):
+            nc.sync.dma_start(
+                out=w_scales[r:P:32, :].bitcast(I32),
+                in_=wqkv_scales[0, r:16:4, :].bitcast(I32),
+            )
+
+        w_words = sbuf.tile([P, 2 * COLS], U8, align_bytes=64)
+        first = 2 * 2 * BANK
+        nc.sync.dma_start(
+            out=w_words[:, :first].bitcast(I32), in_=wqkv_words[0, :, :first].bitcast(I32)
+        )
+        nc.sync.dma_start(
+            out=w_words[:, first:].bitcast(I32), in_=wqkv_words[0, :, first:].bitcast(I32)
+        )
+
+        warm = sbuf.tile([P, 1], F32)
+        nc.scalar.activation(out=warm[:], in_=eps[:], func=ACT.Abs_reciprocal_sqrt)
+        k_gain = sbuf.tile([P, HEAD], BF16)
+        nc.scalar.dma_start(out=k_gain[:], in_=k_norm_w.partition_broadcast(P))
+
+        ident = sbuf.tile([P, P], F32)
+        make_identity(nc, ident[:])
+
+        x_words = x_sb[:].bitcast(F32)
+        xt = psum.tile([P, 2, P], F32)
+        for u in range(2):
+            nc.tensor.transpose(xt[:, u, :], x_words[:, u : K // 2 : 2], ident[:])
+        x_grouped = sbuf.tile([P, 4 * P], BF16, align_bytes=64)
+        nc.vector.tensor_copy(
+            out=x_grouped[:].bitcast(F32).rearrange("p (r u) -> p r u", u=2),
+            in_=xt[:].rearrange("p u r -> p r u"),
+        )
+        x_codes = sbuf.tile([P, P], U32, align_bytes=64)
+        x_scales = sbuf.tile([P, P], U8, align_bytes=64)
+        nc.vector.quantize_mx(
+            out=x_codes[:].bitcast(FP8X4), scales=x_scales[:], in_=x_grouped[:]
+        )
+
+        banks = [psum.tile([P, BANK], F32, name="bank%d" % b) for b in range(N_BANKS)]
+        for b in (0, 1, V_BANK, 2, 3, K_BANK):
+            nc.tensor.matmul_mx(
+                out=banks[b][:],
+                lhsT=x_codes[:].bitcast(FP8X4),
+                lhsT_scale=x_scales[:],
+                rhs=w_words[:, 2 * BANK * b : 2 * BANK * (b + 1)].bitcast(FP4X4),
+                rhs_scale=w_scales[:, BANK * b : BANK * (b + 1)],
+                start=True,
+                stop=True,
+            )
+
+        def rotation_tables(gain, name):
+            fc = fc_sb[:].rearrange("p (j e) -> p j e", e=2)
+            g = gain[:].rearrange("p (j e) -> p j e", e=2)
+            from_even = sbuf.tile([P, PAIRS, 2], F32, name="from_even_" + name)
+            from_odd = sbuf.tile([P, PAIRS, 2], F32, name="from_odd_" + name)
+            nc.vector.tensor_tensor(
+                out=from_even[:], in0=fc, in1=g[:, :, 0:1].to_broadcast([P, PAIRS, 2]), op=ALU.mult
+            )
+            nc.vector.scalar_tensor_tensor(
+                out=from_odd[:, :, 0:1], in0=fc[:, :, 1:2], scalar=-1.0, in1=g[:, :, 1:2],
+                op0=ALU.mult, op1=ALU.mult,
+            )
+            nc.vector.tensor_tensor(
+                out=from_odd[:, :, 1:2], in0=fc[:, :, 0:1], in1=g[:, :, 1:2], op=ALU.mult
+            )
+            return from_even, from_odd
+
+        n_heads = NORMED_BANKS * HEADS_PER_BANK
+        squares = sbuf.tile([P, n_heads, HEAD], F32)
+        sumsq = sbuf.tile([P, n_heads], F32)
+        rstd = sbuf.tile([P, n_heads], F32)
+
+        def inverse_rms(b):
+            heads = slice(HEADS_PER_BANK * b, HEADS_PER_BANK * (b + 1))
+            for i in range(HEADS_PER_BANK):
+                h = HEADS_PER_BANK * b + i
+                nc.scalar.activation(
+                    out=squares[:, h, :],
+                    in_=banks[b][:, HEAD * i : HEAD * (i + 1)],
+                    func=ACT.Square,
+                    accum_out=sumsq[:, h : h + 1],
+                )
+            nc.scalar.activation(
+                out=rstd[:, heads], in_=sumsq[:, heads], func=ACT.Abs_reciprocal_sqrt,
+                scale=1.0 / HEAD, bias=eps[:],
+            )
+
+        def products(b, tables):
+            part_even = sbuf.tile([P, HEADS_PER_BANK, PAIRS, 2], F32, name="part_even%d" % b)
+            part_odd = sbuf.tile([P, HEADS_PER_BANK, PAIRS, 2], F32, name="part_odd%d" % b)
+            for i in range(HEADS_PER_BANK):
+                h = HEADS_PER_BANK * b + i
+                u = banks[b][:, HEAD * i : HEAD * (i + 1)].rearrange("p (j e) -> p j e", e=2)
+                for e, part in enumerate((part_even, part_odd)):
+                    nc.vector.scalar_tensor_tensor(
+                        out=part[:, i, :, :],
+                        in0=u[:, :, e : e + 1].to_broadcast([P, PAIRS, 2]),
+                        scalar=rstd[:, h : h + 1],
+                        in1=tables[e][:],
+                        op0=ALU.mult,
+                        op1=ALU.mult,
+                    )
+            return part_even, part_odd
+
+        def add_and_store(engine, b, parts, dest):
+            rotated = sbuf.tile([P, BANK], F32, name="rotated%d" % b)
+            engine.tensor_tensor(
+                out=rotated[:],
+                in0=parts[0][:].rearrange("p h j e -> p (h j e)"),
+                in1=parts[1][:].rearrange("p h j e -> p (h j e)"),
+                op=ALU.add,
+            )
+            nc.sync.dma_start(out=dest, in_=rotated[:])
+
+        q_tables = rotation_tables(q_gain, "q")
+        k_tables = None
+        for b in range(NORMED_BANKS):
+            inverse_rms(b)
+            if b == 1:
+                v_sb = sbuf.tile([P, BANK], F32)
+                nc.scalar.copy(out=v_sb[:], in_=banks[V_BANK][:])
+                nc.sync.dma_start(out=v_out, in_=v_sb[:])
+                k_tables = rotation_tables(k_gain, "k")
+            if b < Q_BANKS:
+                parts = products(b, q_tables)
+                add_and_store(nc.gpsimd, b, parts, q_out[:, BANK * b : BANK * (b + 1)])
+            else:
+                parts = products(b, k_tables)
+                add_and_store(nc.vector, b, parts, k_out)

@@ -47,13 +47,11 @@ def tile_attention_pa_s_kernel(
         x_sb = sbuf.tile([P, K], BF16)
         nc.sync.dma_start(out=x_sb[:], in_=x.flatten_outer_dims())
 
-        fc_sb = sbuf.tile([P, HEAD], BF16)
-        fc_rows = freqs_cis.rearrange("s j e -> s (j e)")
-        nc.scalar.dma_start(
-            out=fc_sb[:], in_=fc_rows.unsqueeze(0).to_broadcast([P // SEQ, SEQ, HEAD])
+        w_words = sbuf.tile([P, 2 * COLS], U8, align_bytes=64)
+        first = 2 * 2 * BANK
+        nc.sync.dma_start(
+            out=w_words[:, :first].bitcast(I32), in_=wqkv_words[0, :, :first].bitcast(I32)
         )
-        q_gain = sbuf.tile([P, HEAD], BF16)
-        nc.scalar.dma_start(out=q_gain[:], in_=q_norm_w.partition_broadcast(P))
 
         eps = sbuf.tile([P, 1], F32)
         nc.vector.memset(eps[:], EPS)
@@ -64,21 +62,22 @@ def tile_attention_pa_s_kernel(
                 out=w_scales[r:P:32, :].bitcast(I32),
                 in_=wqkv_scales[0, r:16:4, :].bitcast(I32),
             )
-
-        w_words = sbuf.tile([P, 2 * COLS], U8, align_bytes=64)
-        first = 2 * 2 * BANK
-        nc.sync.dma_start(
-            out=w_words[:, :first].bitcast(I32), in_=wqkv_words[0, :, :first].bitcast(I32)
-        )
         nc.sync.dma_start(
             out=w_words[:, first:].bitcast(I32), in_=wqkv_words[0, :, first:].bitcast(I32)
         )
 
+        fc_sb = sbuf.tile([P, PAIRS, 2], BF16)
+        nc.scalar.dma_start(
+            out=fc_sb[:].rearrange("p j e -> p (j e)"),
+            in_=freqs_cis.rearrange("s j e -> s (j e)").unsqueeze(0).to_broadcast([P // SEQ, SEQ, HEAD]),
+        )
         warm = sbuf.tile([P, 1], F32)
         nc.scalar.activation(out=warm[:], in_=eps[:], func=ACT.Abs_reciprocal_sqrt)
         k_gain = sbuf.tile([P, HEAD], BF16)
         nc.scalar.dma_start(out=k_gain[:], in_=k_norm_w.partition_broadcast(P))
 
+        q_gain = sbuf.tile([P, HEAD], BF16)
+        nc.gpsimd.dma_start(out=q_gain[:], in_=q_norm_w.partition_broadcast(P))
         ident = sbuf.tile([P, P], F32)
         make_identity(nc, ident[:])
 
@@ -87,7 +86,7 @@ def tile_attention_pa_s_kernel(
         for u in range(2):
             nc.tensor.transpose(xt[:, u, :], x_words[:, u : K // 2 : 2], ident[:])
         x_grouped = sbuf.tile([P, 4 * P], BF16, align_bytes=64)
-        nc.vector.tensor_copy(
+        nc.scalar.copy(
             out=x_grouped[:].bitcast(F32).rearrange("p (r u) -> p r u", u=2),
             in_=xt[:].rearrange("p u r -> p r u"),
         )
@@ -98,7 +97,7 @@ def tile_attention_pa_s_kernel(
         )
 
         banks = [psum.tile([P, BANK], F32, name="bank%d" % b) for b in range(N_BANKS)]
-        for b in (0, 1, V_BANK, 2, 3, K_BANK):
+        for b in range(N_BANKS):
             nc.tensor.matmul_mx(
                 out=banks[b][:],
                 lhsT=x_codes[:].bitcast(FP8X4),
@@ -109,22 +108,23 @@ def tile_attention_pa_s_kernel(
                 stop=True,
             )
 
-        def rotation_tables(gain, name):
-            fc = fc_sb[:].rearrange("p (j e) -> p j e", e=2)
-            g = gain[:].rearrange("p (j e) -> p j e", e=2)
-            from_even = sbuf.tile([P, PAIRS, 2], F32, name="from_even_" + name)
-            from_odd = sbuf.tile([P, PAIRS, 2], F32, name="from_odd_" + name)
-            nc.vector.tensor_tensor(
-                out=from_even[:], in0=fc, in1=g[:, :, 0:1].to_broadcast([P, PAIRS, 2]), op=ALU.mult
+        rot = sbuf.tile([P, PAIRS, 2, 2], BF16)
+        nc.vector.tensor_copy(out=rot[:, :, 0, :], in_=fc_sb[:])
+        nc.vector.tensor_copy(out=rot[:, :, 1, 1:2], in_=fc_sb[:, :, 0:1])
+        nc.vector.tensor_scalar_mul(out=rot[:, :, 1, 0:1], in0=fc_sb[:, :, 1:2], scalar1=-1.0)
+
+        def rotation_table(engine, gain, name):
+            table = sbuf.tile([P, HEAD, 2], F32, name=name)
+            engine.tensor_tensor(
+                out=table[:],
+                in0=rot[:].rearrange("p j a e -> p (j a) e"),
+                in1=gain[:].unsqueeze(2).to_broadcast([P, HEAD, 2]),
+                op=ALU.mult,
             )
-            nc.vector.scalar_tensor_tensor(
-                out=from_odd[:, :, 0:1], in0=fc[:, :, 1:2], scalar=-1.0, in1=g[:, :, 1:2],
-                op0=ALU.mult, op1=ALU.mult,
-            )
-            nc.vector.tensor_tensor(
-                out=from_odd[:, :, 1:2], in0=fc[:, :, 0:1], in1=g[:, :, 1:2], op=ALU.mult
-            )
-            return from_even, from_odd
+            return table
+
+        q_table = rotation_table(nc.vector, q_gain, "q_table")
+        k_table = rotation_table(nc.gpsimd, k_gain, "k_table")
 
         n_heads = NORMED_BANKS * HEADS_PER_BANK
         squares = sbuf.tile([P, n_heads, HEAD], F32)
@@ -133,58 +133,59 @@ def tile_attention_pa_s_kernel(
 
         def inverse_rms(b):
             heads = slice(HEADS_PER_BANK * b, HEADS_PER_BANK * (b + 1))
-            for i in range(HEADS_PER_BANK):
-                h = HEADS_PER_BANK * b + i
-                nc.scalar.activation(
-                    out=squares[:, h, :],
-                    in_=banks[b][:, HEAD * i : HEAD * (i + 1)],
-                    func=ACT.Square,
-                    accum_out=sumsq[:, h : h + 1],
-                )
             nc.scalar.activation(
                 out=rstd[:, heads], in_=sumsq[:, heads], func=ACT.Abs_reciprocal_sqrt,
                 scale=1.0 / HEAD, bias=eps[:],
             )
 
-        def products(b, tables):
-            part_even = sbuf.tile([P, HEADS_PER_BANK, PAIRS, 2], F32, name="part_even%d" % b)
-            part_odd = sbuf.tile([P, HEADS_PER_BANK, PAIRS, 2], F32, name="part_odd%d" % b)
+        for h in range(n_heads):
+            b, i = divmod(h, HEADS_PER_BANK)
+            nc.scalar.activation(
+                out=squares[:, h, :],
+                in_=banks[b][:, HEAD * i : HEAD * (i + 1)],
+                func=ACT.Square,
+                accum_out=sumsq[:, h : h + 1],
+            )
+            if i == 0 and b > 0:
+                inverse_rms(b - 1)
+        inverse_rms(NORMED_BANKS - 1)
+        v_sb = sbuf.tile([P, BANK], F32)
+        nc.scalar.copy(out=v_sb[:], in_=banks[V_BANK][:])
+
+        def products(b, table):
+            prod = sbuf.tile([P, HEADS_PER_BANK, HEAD, 2], F32, name="prod%d" % b)
             for i in range(HEADS_PER_BANK):
                 h = HEADS_PER_BANK * b + i
-                u = banks[b][:, HEAD * i : HEAD * (i + 1)].rearrange("p (j e) -> p j e", e=2)
-                for e, part in enumerate((part_even, part_odd)):
-                    nc.vector.scalar_tensor_tensor(
-                        out=part[:, i, :, :],
-                        in0=u[:, :, e : e + 1].to_broadcast([P, PAIRS, 2]),
-                        scalar=rstd[:, h : h + 1],
-                        in1=tables[e][:],
-                        op0=ALU.mult,
-                        op1=ALU.mult,
-                    )
-            return part_even, part_odd
+                nc.vector.scalar_tensor_tensor(
+                    out=prod[:, i, :, :],
+                    in0=banks[b][:, HEAD * i : HEAD * (i + 1)].unsqueeze(2).to_broadcast([P, HEAD, 2]),
+                    scalar=rstd[:, h : h + 1],
+                    in1=table[:],
+                    op0=ALU.mult,
+                    op1=ALU.mult,
+                )
+            return prod
 
-        def add_and_store(engine, b, parts, dest):
-            rotated = sbuf.tile([P, BANK], F32, name="rotated%d" % b)
+        def add_and_store(engine, prod, rotated, head0, head1, dest):
+            pairs = prod[:, head0:head1, :, :].rearrange("p h (j a) e -> p (h j) a e", a=2)
+            cols = slice(HEAD * head0, HEAD * head1)
             engine.tensor_tensor(
-                out=rotated[:],
-                in0=parts[0][:].rearrange("p h j e -> p (h j e)"),
-                in1=parts[1][:].rearrange("p h j e -> p (h j e)"),
+                out=rotated[:, cols].rearrange("p (n e) -> p n e", e=2),
+                in0=pairs[:, :, 0, :],
+                in1=pairs[:, :, 1, :],
                 op=ALU.add,
             )
-            nc.sync.dma_start(out=dest, in_=rotated[:])
+            nc.sync.dma_start(out=dest[:, cols], in_=rotated[:, cols])
 
-        q_tables = rotation_tables(q_gain, "q")
-        k_tables = None
-        for b in range(NORMED_BANKS):
-            inverse_rms(b)
+        for b in range(Q_BANKS):
+            prod = products(b, q_table)
+            rotated = sbuf.tile([P, BANK], F32, name="rotated%d" % b)
+            add_and_store(
+                nc.gpsimd, prod, rotated, 0, HEADS_PER_BANK, q_out[:, BANK * b : BANK * (b + 1)]
+            )
             if b == 1:
-                v_sb = sbuf.tile([P, BANK], F32)
-                nc.scalar.copy(out=v_sb[:], in_=banks[V_BANK][:])
                 nc.sync.dma_start(out=v_out, in_=v_sb[:])
-                k_tables = rotation_tables(k_gain, "k")
-            if b < Q_BANKS:
-                parts = products(b, q_tables)
-                add_and_store(nc.gpsimd, b, parts, q_out[:, BANK * b : BANK * (b + 1)])
-            else:
-                parts = products(b, k_tables)
-                add_and_store(nc.vector, b, parts, k_out)
+        prod = products(K_BANK, k_table)
+        rotated = sbuf.tile([P, BANK], F32, name="rotated%d" % K_BANK)
+        for half in range(2):
+            add_and_store(nc.vector, prod, rotated, 2 * half, 2 * half + 2, k_out)

@@ -53,8 +53,13 @@ def tile_attention_pa_s_kernel(
             out=w_words[:, :first].bitcast(I32), in_=wqkv_words[0, :, :first].bitcast(I32)
         )
 
+        gain_rows = sbuf.tile([P, 2, HEAD], BF16)
+        nc.vector.memset(gain_rows[:], 0.0)
         eps = sbuf.tile([P, 1], F32)
         nc.vector.memset(eps[:], EPS)
+        nc.scalar.dma_start(out=gain_rows[0:1, 0, :], in_=q_norm_w.unsqueeze(0))
+        nc.scalar.dma_start(out=gain_rows[0:1, 1, :], in_=k_norm_w.unsqueeze(0))
+
         w_scales = sbuf.tile([P, COLS], U8, align_bytes=64)
         nc.vector.memset(w_scales[:].bitcast(I32), 0)
         for r in range(4):
@@ -65,19 +70,17 @@ def tile_attention_pa_s_kernel(
         nc.sync.dma_start(
             out=w_words[:, first:].bitcast(I32), in_=wqkv_words[0, :, first:].bitcast(I32)
         )
+        ones = sbuf.tile([P, P], BF16)
+        nc.vector.memset(ones[:], 1.0)
+
+        warm = sbuf.tile([P, 1], F32)
+        nc.scalar.activation(out=warm[:], in_=eps[:], func=ACT.Abs_reciprocal_sqrt)
 
         fc_sb = sbuf.tile([P, PAIRS, 2], BF16)
-        nc.scalar.dma_start(
+        nc.gpsimd.dma_start(
             out=fc_sb[:].rearrange("p j e -> p (j e)"),
             in_=freqs_cis.rearrange("s j e -> s (j e)").unsqueeze(0).to_broadcast([P // SEQ, SEQ, HEAD]),
         )
-        warm = sbuf.tile([P, 1], F32)
-        nc.scalar.activation(out=warm[:], in_=eps[:], func=ACT.Abs_reciprocal_sqrt)
-        k_gain = sbuf.tile([P, HEAD], BF16)
-        nc.scalar.dma_start(out=k_gain[:], in_=k_norm_w.partition_broadcast(P))
-
-        q_gain = sbuf.tile([P, HEAD], BF16)
-        nc.gpsimd.dma_start(out=q_gain[:], in_=q_norm_w.partition_broadcast(P))
         ident = sbuf.tile([P, P], F32)
         make_identity(nc, ident[:])
 
@@ -94,6 +97,15 @@ def tile_attention_pa_s_kernel(
         x_scales = sbuf.tile([P, P], U8, align_bytes=64)
         nc.vector.quantize_mx(
             out=x_codes[:].bitcast(FP8X4), scales=x_scales[:], in_=x_grouped[:]
+        )
+
+        gains = psum.tile([P, 2, HEAD], F32)
+        nc.tensor.matmul(
+            out=gains[:].rearrange("p w c -> p (w c)"),
+            lhsT=ones[:],
+            rhs=gain_rows[:].rearrange("p w c -> p (w c)"),
+            start=True,
+            stop=True,
         )
 
         banks = [psum.tile([P, BANK], F32, name="bank%d" % b) for b in range(N_BANKS)]
@@ -113,18 +125,13 @@ def tile_attention_pa_s_kernel(
         nc.vector.tensor_copy(out=rot[:, :, 1, 1:2], in_=fc_sb[:, :, 0:1])
         nc.vector.tensor_scalar_mul(out=rot[:, :, 1, 0:1], in0=fc_sb[:, :, 1:2], scalar1=-1.0)
 
-        def rotation_table(engine, gain, name):
-            table = sbuf.tile([P, HEAD, 2], F32, name=name)
-            engine.tensor_tensor(
-                out=table[:],
-                in0=rot[:].rearrange("p j a e -> p (j a) e"),
-                in1=gain[:].unsqueeze(2).to_broadcast([P, HEAD, 2]),
-                op=ALU.mult,
-            )
-            return table
-
-        q_table = rotation_table(nc.vector, q_gain, "q_table")
-        k_table = rotation_table(nc.gpsimd, k_gain, "k_table")
+        tables = sbuf.tile([P, 2, HEAD, 2], F32)
+        nc.vector.tensor_tensor(
+            out=tables[:],
+            in0=rot[:].rearrange("p j a e -> p (j a) e").unsqueeze(1).to_broadcast([P, 2, HEAD, 2]),
+            in1=gains[:].unsqueeze(3).to_broadcast([P, 2, HEAD, 2]),
+            op=ALU.mult,
+        )
 
         n_heads = NORMED_BANKS * HEADS_PER_BANK
         squares = sbuf.tile([P, n_heads, HEAD], F32)
@@ -160,7 +167,7 @@ def tile_attention_pa_s_kernel(
                     out=prod[:, i, :, :],
                     in0=banks[b][:, HEAD * i : HEAD * (i + 1)].unsqueeze(2).to_broadcast([P, HEAD, 2]),
                     scalar=rstd[:, h : h + 1],
-                    in1=table[:],
+                    in1=table,
                     op0=ALU.mult,
                     op1=ALU.mult,
                 )
@@ -178,14 +185,14 @@ def tile_attention_pa_s_kernel(
             nc.sync.dma_start(out=dest[:, cols], in_=rotated[:, cols])
 
         for b in range(Q_BANKS):
-            prod = products(b, q_table)
+            prod = products(b, tables[:, 0, :, :])
             rotated = sbuf.tile([P, BANK], F32, name="rotated%d" % b)
             add_and_store(
                 nc.gpsimd, prod, rotated, 0, HEADS_PER_BANK, q_out[:, BANK * b : BANK * (b + 1)]
             )
             if b == 1:
                 nc.sync.dma_start(out=v_out, in_=v_sb[:])
-        prod = products(K_BANK, k_table)
+        prod = products(K_BANK, tables[:, 1, :, :])
         rotated = sbuf.tile([P, BANK], F32, name="rotated%d" % K_BANK)
         for half in range(2):
             add_and_store(nc.vector, prod, rotated, 2 * half, 2 * half + 2, k_out)

@@ -49,10 +49,9 @@ def tile_attention_pa_s_kernel(
 
         w_words = sbuf.tile([P, 2 * COLS], U8, align_bytes=64)
         first = 2 * 2 * BANK
-        nc.sync.dma_start(
-            out=w_words[:, :first].bitcast(I32), in_=wqkv_words[0, :, :first].bitcast(I32)
-        )
 
+        w_scales = sbuf.tile([P, COLS], U8, align_bytes=64)
+        nc.vector.memset(w_scales[:].bitcast(I32), 0)
         gain_rows = sbuf.tile([P, 2, HEAD], BF16)
         nc.vector.memset(gain_rows[:], 0.0)
         eps = sbuf.tile([P, 1], F32)
@@ -60,13 +59,14 @@ def tile_attention_pa_s_kernel(
         nc.scalar.dma_start(out=gain_rows[0:1, 0, :], in_=q_norm_w.unsqueeze(0))
         nc.scalar.dma_start(out=gain_rows[0:1, 1, :], in_=k_norm_w.unsqueeze(0))
 
-        w_scales = sbuf.tile([P, COLS], U8, align_bytes=64)
-        nc.vector.memset(w_scales[:].bitcast(I32), 0)
         for r in range(4):
             nc.sync.dma_start(
                 out=w_scales[r:P:32, :].bitcast(I32),
                 in_=wqkv_scales[0, r:16:4, :].bitcast(I32),
             )
+        nc.sync.dma_start(
+            out=w_words[:, :first].bitcast(I32), in_=wqkv_words[0, :, :first].bitcast(I32)
+        )
         nc.sync.dma_start(
             out=w_words[:, first:].bitcast(I32), in_=wqkv_words[0, :, first:].bitcast(I32)
         )

@@ -49,38 +49,35 @@ def tile_attention_pa_s_kernel(
 
         w_words = sbuf.tile([P, 2 * COLS], U8, align_bytes=64)
         first = 2 * 2 * BANK
+        nc.sync.dma_start(
+            out=w_words[:, :first].bitcast(I32), in_=wqkv_words[0, :, :first].bitcast(I32)
+        )
 
-        w_scales = sbuf.tile([P, COLS], U8, align_bytes=64)
-        nc.vector.memset(w_scales[:].bitcast(I32), 0)
-        gain_rows = sbuf.tile([P, 2, HEAD], BF16)
-        nc.vector.memset(gain_rows[:], 0.0)
         eps = sbuf.tile([P, 1], F32)
         nc.vector.memset(eps[:], EPS)
-        nc.scalar.dma_start(out=gain_rows[0:1, 0, :], in_=q_norm_w.unsqueeze(0))
-        nc.scalar.dma_start(out=gain_rows[0:1, 1, :], in_=k_norm_w.unsqueeze(0))
-
+        w_scales = sbuf.tile([P, COLS], U8, align_bytes=64)
+        nc.vector.memset(w_scales[:].bitcast(I32), 0)
         for r in range(4):
             nc.sync.dma_start(
                 out=w_scales[r:P:32, :].bitcast(I32),
                 in_=wqkv_scales[0, r:16:4, :].bitcast(I32),
             )
         nc.sync.dma_start(
-            out=w_words[:, :first].bitcast(I32), in_=wqkv_words[0, :, :first].bitcast(I32)
-        )
-        nc.sync.dma_start(
             out=w_words[:, first:].bitcast(I32), in_=wqkv_words[0, :, first:].bitcast(I32)
         )
-        ones = sbuf.tile([P, P], BF16)
-        nc.vector.memset(ones[:], 1.0)
-
-        warm = sbuf.tile([P, 1], F32)
-        nc.scalar.activation(out=warm[:], in_=eps[:], func=ACT.Abs_reciprocal_sqrt)
 
         fc_sb = sbuf.tile([P, PAIRS, 2], BF16)
-        nc.gpsimd.dma_start(
+        nc.scalar.dma_start(
             out=fc_sb[:].rearrange("p j e -> p (j e)"),
             in_=freqs_cis.rearrange("s j e -> s (j e)").unsqueeze(0).to_broadcast([P // SEQ, SEQ, HEAD]),
         )
+        q_gain = sbuf.tile([P, HEAD], BF16)
+        nc.scalar.dma_start(out=q_gain[:], in_=q_norm_w.partition_broadcast(P))
+        warm = sbuf.tile([P, 1], F32)
+        nc.scalar.activation(out=warm[:], in_=eps[:], func=ACT.Abs_reciprocal_sqrt)
+        k_gain = sbuf.tile([P, HEAD], BF16)
+        nc.scalar.dma_start(out=k_gain[:], in_=k_norm_w.partition_broadcast(P))
+
         ident = sbuf.tile([P, P], F32)
         make_identity(nc, ident[:])
 
@@ -97,15 +94,6 @@ def tile_attention_pa_s_kernel(
         x_scales = sbuf.tile([P, P], U8, align_bytes=64)
         nc.vector.quantize_mx(
             out=x_codes[:].bitcast(FP8X4), scales=x_scales[:], in_=x_grouped[:]
-        )
-
-        gains = psum.tile([P, 2, HEAD], F32)
-        nc.tensor.matmul(
-            out=gains[:].rearrange("p w c -> p (w c)"),
-            lhsT=ones[:],
-            rhs=gain_rows[:].rearrange("p w c -> p (w c)"),
-            start=True,
-            stop=True,
         )
 
         banks = [psum.tile([P, BANK], F32, name="bank%d" % b) for b in range(N_BANKS)]
@@ -125,13 +113,18 @@ def tile_attention_pa_s_kernel(
         nc.vector.tensor_copy(out=rot[:, :, 1, 1:2], in_=fc_sb[:, :, 0:1])
         nc.vector.tensor_scalar_mul(out=rot[:, :, 1, 0:1], in0=fc_sb[:, :, 1:2], scalar1=-1.0)
 
-        tables = sbuf.tile([P, 2, HEAD, 2], F32)
-        nc.vector.tensor_tensor(
-            out=tables[:],
-            in0=rot[:].rearrange("p j a e -> p (j a) e").unsqueeze(1).to_broadcast([P, 2, HEAD, 2]),
-            in1=gains[:].unsqueeze(3).to_broadcast([P, 2, HEAD, 2]),
-            op=ALU.mult,
-        )
+        def rotation_table(engine, gain, name):
+            table = sbuf.tile([P, HEAD, 2], F32, name=name)
+            engine.tensor_tensor(
+                out=table[:],
+                in0=rot[:].rearrange("p j a e -> p (j a) e"),
+                in1=gain[:].unsqueeze(2).to_broadcast([P, HEAD, 2]),
+                op=ALU.mult,
+            )
+            return table
+
+        q_table = rotation_table(nc.vector, q_gain, "q_table")
+        k_table = rotation_table(nc.gpsimd, k_gain, "k_table")
 
         n_heads = NORMED_BANKS * HEADS_PER_BANK
         squares = sbuf.tile([P, n_heads, HEAD], F32)
@@ -167,7 +160,7 @@ def tile_attention_pa_s_kernel(
                     out=prod[:, i, :, :],
                     in0=banks[b][:, HEAD * i : HEAD * (i + 1)].unsqueeze(2).to_broadcast([P, HEAD, 2]),
                     scalar=rstd[:, h : h + 1],
-                    in1=table,
+                    in1=table[:],
                     op0=ALU.mult,
                     op1=ALU.mult,
                 )
@@ -185,14 +178,14 @@ def tile_attention_pa_s_kernel(
             nc.sync.dma_start(out=dest[:, cols], in_=rotated[:, cols])
 
         for b in range(Q_BANKS):
-            prod = products(b, tables[:, 0, :, :])
+            prod = products(b, q_table)
             rotated = sbuf.tile([P, BANK], F32, name="rotated%d" % b)
             add_and_store(
                 nc.gpsimd, prod, rotated, 0, HEADS_PER_BANK, q_out[:, BANK * b : BANK * (b + 1)]
             )
             if b == 1:
                 nc.sync.dma_start(out=v_out, in_=v_sb[:])
-        prod = products(K_BANK, tables[:, 1, :, :])
+        prod = products(K_BANK, k_table)
         rotated = sbuf.tile([P, BANK], F32, name="rotated%d" % K_BANK)
         for half in range(2):
             add_and_store(nc.vector, prod, rotated, 2 * half, 2 * half + 2, k_out)

@@ -18,14 +18,15 @@ SEQ = 64
 K = 512
 HEAD = 128
 PAIRS = HEAD // 2
-BANK = 512
-HEADS_PER_BANK = BANK // HEAD
-Q_BANKS = 4
-K_BANK = 4
-V_BANK = 5
-NORMED_BANKS = Q_BANKS + 1
-N_BANKS = 6
-COLS = N_BANKS * BANK
+Q_HEADS = 16
+K_HEADS = 4
+V_HEADS = 4
+NORMED_HEADS = Q_HEADS + K_HEADS
+COLS = (NORMED_HEADS + V_HEADS) * HEAD
+PASS_HEADS = (2, 2, 4, 4, 4, 4, 4)
+GROUP = 2
+N_GROUPS = NORMED_HEADS // GROUP
+V_STORE_GROUP = 7
 EPS = 1e-6
 
 FLOPS = 2 * P * K * COLS
@@ -48,9 +49,9 @@ def tile_attention_pa_s_kernel(
         nc.sync.dma_start(out=x_sb[:], in_=x.flatten_outer_dims())
 
         w_words = sbuf.tile([P, 2 * COLS], U8, align_bytes=64)
-        first = 2 * 2 * BANK
+        q_bytes = 2 * Q_HEADS * HEAD
         nc.sync.dma_start(
-            out=w_words[:, :first].bitcast(I32), in_=wqkv_words[0, :, :first].bitcast(I32)
+            out=w_words[:, :q_bytes].bitcast(I32), in_=wqkv_words[0, :, :q_bytes].bitcast(I32)
         )
 
         eps = sbuf.tile([P, 1], F32)
@@ -63,7 +64,7 @@ def tile_attention_pa_s_kernel(
                 in_=wqkv_scales[0, r:16:4, :].bitcast(I32),
             )
         nc.sync.dma_start(
-            out=w_words[:, first:].bitcast(I32), in_=wqkv_words[0, :, first:].bitcast(I32)
+            out=w_words[:, q_bytes:].bitcast(I32), in_=wqkv_words[0, :, q_bytes:].bitcast(I32)
         )
 
         fc_sb = sbuf.tile([P, PAIRS, 2], BF16)
@@ -96,17 +97,21 @@ def tile_attention_pa_s_kernel(
             out=x_codes[:].bitcast(FP8X4), scales=x_scales[:], in_=x_grouped[:]
         )
 
-        banks = [psum.tile([P, BANK], F32, name="bank%d" % b) for b in range(N_BANKS)]
-        for b in range(N_BANKS):
+        head_sums = []
+        for n in PASS_HEADS:
+            head0 = len(head_sums)
+            acc = psum.tile([P, n, HEAD], F32, name="acc%d" % head0)
             nc.tensor.matmul_mx(
-                out=banks[b][:],
+                out=acc[:].rearrange("p n c -> p (n c)"),
                 lhsT=x_codes[:].bitcast(FP8X4),
                 lhsT_scale=x_scales[:],
-                rhs=w_words[:, 2 * BANK * b : 2 * BANK * (b + 1)].bitcast(FP4X4),
-                rhs_scale=w_scales[:, BANK * b : BANK * (b + 1)],
+                rhs=w_words[:, 2 * HEAD * head0 : 2 * HEAD * (head0 + n)].bitcast(FP4X4),
+                rhs_scale=w_scales[:, HEAD * head0 : HEAD * (head0 + n)],
                 start=True,
                 stop=True,
             )
+            head_sums.extend([acc[:, i, :] for i in range(n)])
+        v_sums = acc
 
         rot = sbuf.tile([P, PAIRS, 2, 2], BF16)
         nc.vector.tensor_copy(out=rot[:, :, 0, :], in_=fc_sb[:])
@@ -126,66 +131,60 @@ def tile_attention_pa_s_kernel(
         q_table = rotation_table(nc.vector, q_gain, "q_table")
         k_table = rotation_table(nc.gpsimd, k_gain, "k_table")
 
-        n_heads = NORMED_BANKS * HEADS_PER_BANK
-        squares = sbuf.tile([P, n_heads, HEAD], F32)
-        sumsq = sbuf.tile([P, n_heads], F32)
-        rstd = sbuf.tile([P, n_heads], F32)
+        squares = sbuf.tile([P, NORMED_HEADS, HEAD], F32)
+        sumsq = sbuf.tile([P, NORMED_HEADS], F32)
+        rstd = sbuf.tile([P, NORMED_HEADS], F32)
 
-        def inverse_rms(b):
-            heads = slice(HEADS_PER_BANK * b, HEADS_PER_BANK * (b + 1))
+        def inverse_rms(g):
+            heads = slice(GROUP * g, GROUP * (g + 1))
             nc.scalar.activation(
                 out=rstd[:, heads], in_=sumsq[:, heads], func=ACT.Abs_reciprocal_sqrt,
                 scale=1.0 / HEAD, bias=eps[:],
             )
 
-        for h in range(n_heads):
-            b, i = divmod(h, HEADS_PER_BANK)
+        for h in range(NORMED_HEADS):
             nc.scalar.activation(
-                out=squares[:, h, :],
-                in_=banks[b][:, HEAD * i : HEAD * (i + 1)],
-                func=ACT.Square,
+                out=squares[:, h, :], in_=head_sums[h], func=ACT.Square,
                 accum_out=sumsq[:, h : h + 1],
             )
-            if i == 0 and b > 0:
-                inverse_rms(b - 1)
-        inverse_rms(NORMED_BANKS - 1)
-        v_sb = sbuf.tile([P, BANK], F32)
-        nc.scalar.copy(out=v_sb[:], in_=banks[V_BANK][:])
+            if h % GROUP == 0 and h > 0:
+                inverse_rms(h // GROUP - 1)
+        inverse_rms(N_GROUPS - 1)
+        v_sb = sbuf.tile([P, V_HEADS * HEAD], F32)
+        nc.scalar.copy(out=v_sb[:], in_=v_sums[:].rearrange("p n c -> p (n c)"))
 
-        def products(b, table):
-            prod = sbuf.tile([P, HEADS_PER_BANK, HEAD, 2], F32, name="prod%d" % b)
-            for i in range(HEADS_PER_BANK):
-                h = HEADS_PER_BANK * b + i
+        def products(g):
+            prod = sbuf.tile([P, GROUP, HEAD, 2], F32, name="prod%d" % g)
+            for i in range(GROUP):
+                h = GROUP * g + i
                 nc.vector.scalar_tensor_tensor(
                     out=prod[:, i, :, :],
-                    in0=banks[b][:, HEAD * i : HEAD * (i + 1)].unsqueeze(2).to_broadcast([P, HEAD, 2]),
+                    in0=head_sums[h].unsqueeze(2).to_broadcast([P, HEAD, 2]),
                     scalar=rstd[:, h : h + 1],
-                    in1=table[:],
+                    in1=(q_table if h < Q_HEADS else k_table)[:],
                     op0=ALU.mult,
                     op1=ALU.mult,
                 )
             return prod
 
-        def add_and_store(engine, prod, rotated, head0, head1, dest):
-            pairs = prod[:, head0:head1, :, :].rearrange("p h (j a) e -> p (h j) a e", a=2)
-            cols = slice(HEAD * head0, HEAD * head1)
-            engine.tensor_tensor(
-                out=rotated[:, cols].rearrange("p (n e) -> p n e", e=2),
-                in0=pairs[:, :, 0, :],
-                in1=pairs[:, :, 1, :],
-                op=ALU.add,
+        def add_and_store(g, prod):
+            pairs = prod[:].rearrange("p h (j a) e -> p (h j) a e", a=2)
+            rotated = sbuf.tile([P, GROUP * PAIRS, 2], F32, name="rotated%d" % g)
+            nc.vector.tensor_tensor(
+                out=rotated[:], in0=pairs[:, :, 0, :], in1=pairs[:, :, 1, :], op=ALU.add
             )
-            nc.sync.dma_start(out=dest[:, cols], in_=rotated[:, cols])
+            head0 = GROUP * g
+            if head0 < Q_HEADS:
+                dest = q_out[:, HEAD * head0 : HEAD * (head0 + GROUP)]
+            else:
+                dest = k_out[:, HEAD * (head0 - Q_HEADS) : HEAD * (head0 - Q_HEADS + GROUP)]
+            nc.sync.dma_start(out=dest, in_=rotated[:].rearrange("p n e -> p (n e)"))
 
-        for b in range(Q_BANKS):
-            prod = products(b, q_table)
-            rotated = sbuf.tile([P, BANK], F32, name="rotated%d" % b)
-            add_and_store(
-                nc.gpsimd, prod, rotated, 0, HEADS_PER_BANK, q_out[:, BANK * b : BANK * (b + 1)]
-            )
-            if b == 1:
+        prods = []
+        for g in range(N_GROUPS):
+            prods.append(products(g))
+            if g > 0:
+                add_and_store(g - 1, prods[g - 1])
+            if g == V_STORE_GROUP:
                 nc.sync.dma_start(out=v_out, in_=v_sb[:])
-        prod = products(K_BANK, k_table)
-        rotated = sbuf.tile([P, BANK], F32, name="rotated%d" % K_BANK)
-        for half in range(2):
-            add_and_store(nc.vector, prod, rotated, 2 * half, 2 * half + 2, k_out)
+        add_and_store(N_GROUPS - 1, prods[N_GROUPS - 1])

@@ -14,6 +14,7 @@ ACT = mybir.ActivationFunctionType
 ALU = mybir.AluOpType
 
 P = 128
+BATCH = 2
 SEQ = 64
 K = 512
 HEAD = 128
@@ -24,9 +25,10 @@ V_HEADS = 4
 NORMED_HEADS = Q_HEADS + K_HEADS
 COLS = (NORMED_HEADS + V_HEADS) * HEAD
 PASS_HEADS = (2, 2, 4, 4, 4, 4, 4)
+N_Q_PASSES = 5
+K_PASS = 5
 GROUP = 2
 N_GROUPS = NORMED_HEADS // GROUP
-V_STORE_GROUP = 7
 EPS = 1e-6
 
 FLOPS = 2 * P * K * COLS
@@ -36,9 +38,11 @@ def tile_attention_pa_s_kernel(
     tc, x, freqs_cis, wqkv_words, wqkv_scales, q_norm_w, k_norm_w, out_0, out_1, out_2
 ):
     nc = tc.nc
-    q_out = out_0.rearrange("b s h d -> (b s) (h d)")
-    k_out = out_1.rearrange("b s h d -> (b s) (h d)")
-    v_out = out_2.rearrange("b s h d -> (b s) (h d)")
+    x_rows = x.rearrange("b s k -> s b k")
+    fc_rows = freqs_cis.rearrange("s j e -> s (j e)").unsqueeze(1).to_broadcast([SEQ, BATCH, HEAD])
+    q_out = out_0.rearrange("b s h d -> s b (h d)")
+    k_out = out_1.rearrange("b s h d -> s b (h d)")
+    v_out = out_2.rearrange("b s h d -> s b (h d)")
 
     with ExitStack() as ctx:
         sbuf = ctx.enter_context(tc.tile_pool(name="sbuf", bufs=1))
@@ -46,7 +50,7 @@ def tile_attention_pa_s_kernel(
         ctx.enter_context(tc.manual_schedule())
 
         x_sb = sbuf.tile([P, K], BF16)
-        nc.sync.dma_start(out=x_sb[:], in_=x.flatten_outer_dims())
+        nc.sync.dma_start(out=x_sb[:], in_=x_rows)
 
         w_words = sbuf.tile([P, 2 * COLS], U8, align_bytes=64)
         q_bytes = 2 * Q_HEADS * HEAD
@@ -63,21 +67,18 @@ def tile_attention_pa_s_kernel(
                 out=w_scales[r:P:32, :].bitcast(I32),
                 in_=wqkv_scales[0, r:16:4, :].bitcast(I32),
             )
+        k_gain = sbuf.tile([P, HEAD], BF16)
+        nc.sync.dma_start(out=k_gain[:], in_=k_norm_w.partition_broadcast(P))
         nc.sync.dma_start(
             out=w_words[:, q_bytes:].bitcast(I32), in_=wqkv_words[0, :, q_bytes:].bitcast(I32)
         )
 
         fc_sb = sbuf.tile([P, PAIRS, 2], BF16)
-        nc.scalar.dma_start(
-            out=fc_sb[:].rearrange("p j e -> p (j e)"),
-            in_=freqs_cis.rearrange("s j e -> s (j e)").unsqueeze(0).to_broadcast([P // SEQ, SEQ, HEAD]),
-        )
+        nc.scalar.dma_start(out=fc_sb[:].rearrange("p j e -> p (j e)"), in_=fc_rows)
         q_gain = sbuf.tile([P, HEAD], BF16)
         nc.scalar.dma_start(out=q_gain[:], in_=q_norm_w.partition_broadcast(P))
         warm = sbuf.tile([P, 1], F32)
         nc.scalar.activation(out=warm[:], in_=eps[:], func=ACT.Abs_reciprocal_sqrt)
-        k_gain = sbuf.tile([P, HEAD], BF16)
-        nc.scalar.dma_start(out=k_gain[:], in_=k_norm_w.partition_broadcast(P))
 
         ident = sbuf.tile([P, P], F32)
         make_identity(nc, ident[:])
@@ -97,9 +98,9 @@ def tile_attention_pa_s_kernel(
             out=x_codes[:].bitcast(FP8X4), scales=x_scales[:], in_=x_grouped[:]
         )
 
-        head_sums = []
-        for n in PASS_HEADS:
-            head0 = len(head_sums)
+        first_head = [sum(PASS_HEADS[:i]) for i in range(len(PASS_HEADS))]
+        sums = []
+        for head0, n in zip(first_head, PASS_HEADS):
             acc = psum.tile([P, n, HEAD], F32, name="acc%d" % head0)
             nc.tensor.matmul_mx(
                 out=acc[:].rearrange("p n c -> p (n c)"),
@@ -110,8 +111,9 @@ def tile_attention_pa_s_kernel(
                 start=True,
                 stop=True,
             )
-            head_sums.extend([acc[:, i, :] for i in range(n)])
-        v_sums = acc
+            sums.append(acc)
+        head_sums = [acc[:, i, :] for acc, n in zip(sums, PASS_HEADS) for i in range(n)]
+        v_sums = sums[K_PASS + 1]
 
         rot = sbuf.tile([P, PAIRS, 2, 2], BF16)
         nc.vector.tensor_copy(out=rot[:, :, 0, :], in_=fc_sb[:])
@@ -153,38 +155,39 @@ def tile_attention_pa_s_kernel(
         v_sb = sbuf.tile([P, V_HEADS * HEAD], F32)
         nc.scalar.copy(out=v_sb[:], in_=v_sums[:].rearrange("p n c -> p (n c)"))
 
-        def products(g):
-            prod = sbuf.tile([P, GROUP, HEAD, 2], F32, name="prod%d" % g)
-            for i in range(GROUP):
-                h = GROUP * g + i
+        def products(i, table):
+            prod = sbuf.tile([P, PASS_HEADS[i], HEAD, 2], F32, name="prod%d" % i)
+            for m in range(PASS_HEADS[i]):
+                h = first_head[i] + m
                 nc.vector.scalar_tensor_tensor(
-                    out=prod[:, i, :, :],
+                    out=prod[:, m, :, :],
                     in0=head_sums[h].unsqueeze(2).to_broadcast([P, HEAD, 2]),
                     scalar=rstd[:, h : h + 1],
-                    in1=(q_table if h < Q_HEADS else k_table)[:],
+                    in1=table[:],
                     op0=ALU.mult,
                     op1=ALU.mult,
                 )
             return prod
 
-        def add_and_store(g, prod):
-            pairs = prod[:].rearrange("p h (j a) e -> p (h j) a e", a=2)
-            rotated = sbuf.tile([P, GROUP * PAIRS, 2], F32, name="rotated%d" % g)
-            nc.vector.tensor_tensor(
+        def add_and_store(engine, prod, m0, m1, dest, name):
+            pairs = prod[:, m0:m1, :, :].rearrange("p h (j a) e -> p (h j) a e", a=2)
+            rotated = sbuf.tile([P, (m1 - m0) * PAIRS, 2], F32, name=name)
+            engine.tensor_tensor(
                 out=rotated[:], in0=pairs[:, :, 0, :], in1=pairs[:, :, 1, :], op=ALU.add
             )
-            head0 = GROUP * g
-            if head0 < Q_HEADS:
-                dest = q_out[:, HEAD * head0 : HEAD * (head0 + GROUP)]
-            else:
-                dest = k_out[:, HEAD * (head0 - Q_HEADS) : HEAD * (head0 - Q_HEADS + GROUP)]
             nc.sync.dma_start(out=dest, in_=rotated[:].rearrange("p n e -> p (n e)"))
 
-        prods = []
-        for g in range(N_GROUPS):
-            prods.append(products(g))
-            if g > 0:
-                add_and_store(g - 1, prods[g - 1])
-            if g == V_STORE_GROUP:
+        for i in range(N_Q_PASSES):
+            n = PASS_HEADS[i]
+            prod = products(i, q_table)
+            add_and_store(
+                nc.gpsimd, prod, 0, n,
+                q_out[:, :, HEAD * first_head[i] : HEAD * (first_head[i] + n)], "q_rot%d" % i,
+            )
+            if i == N_Q_PASSES - 2:
                 nc.sync.dma_start(out=v_out, in_=v_sb[:])
-        add_and_store(N_GROUPS - 1, prods[N_GROUPS - 1])
+        prod = products(K_PASS, k_table)
+        for m0 in range(0, K_HEADS, GROUP):
+            add_and_store(
+                nc.vector, prod, m0, m0 + GROUP, k_out[:, :, HEAD * m0 : HEAD * (m0 + GROUP)], "k_rot%d" % m0
+            )

@@ -16,22 +16,22 @@ ALU = mybir.AluOpType
 P = 128
 BATCH = 2
 SEQ = 64
-K = 512
+DIM = 512
 HEAD = 128
 PAIRS = HEAD // 2
-Q_HEADS = 16
-K_HEADS = 4
-V_HEADS = 4
-NORMED_HEADS = Q_HEADS + K_HEADS
-COLS = (NORMED_HEADS + V_HEADS) * HEAD
+QUERY_HEADS = 16
+KEY_HEADS = 4
+VALUE_HEADS = 4
+NORMED_HEADS = QUERY_HEADS + KEY_HEADS
+COLS = (NORMED_HEADS + VALUE_HEADS) * HEAD
 PASS_HEADS = (2, 2, 4, 4, 4, 4, 4)
-N_Q_PASSES = 5
-K_PASS = 5
+LAST_QUERY_PASS = 4
+KEY_PASS = 5
+VALUE_PASS = 6
 GROUP = 2
-N_GROUPS = NORMED_HEADS // GROUP
 EPS = 1e-6
 
-FLOPS = 2 * P * K * COLS
+FLOPS = 2 * P * DIM * COLS
 
 
 def tile_attention_pa_s_kernel(
@@ -40,22 +40,23 @@ def tile_attention_pa_s_kernel(
     nc = tc.nc
     x_rows = x.rearrange("b s k -> s b k")
     fc_rows = freqs_cis.rearrange("s j e -> s (j e)").unsqueeze(1).to_broadcast([SEQ, BATCH, HEAD])
-    q_out = out_0.rearrange("b s h d -> s b (h d)")
-    k_out = out_1.rearrange("b s h d -> s b (h d)")
-    v_out = out_2.rearrange("b s h d -> s b (h d)")
+    query_out = out_0.rearrange("b s h d -> s b (h d)")
+    key_out = out_1.rearrange("b s h d -> s b (h d)")
+    value_out = out_2.rearrange("b s h d -> s b (h d)")
 
     with ExitStack() as ctx:
         sbuf = ctx.enter_context(tc.tile_pool(name="sbuf", bufs=1))
         psum = ctx.enter_context(tc.psum_pool(name="psum", bufs=1))
         ctx.enter_context(tc.manual_schedule())
 
-        x_sb = sbuf.tile([P, K], BF16)
+        x_sb = sbuf.tile([P, DIM], BF16)
         nc.sync.dma_start(out=x_sb[:], in_=x_rows)
 
         w_words = sbuf.tile([P, 2 * COLS], U8, align_bytes=64)
-        q_bytes = 2 * Q_HEADS * HEAD
+        query_bytes = 2 * QUERY_HEADS * HEAD
         nc.sync.dma_start(
-            out=w_words[:, :q_bytes].bitcast(I32), in_=wqkv_words[0, :, :q_bytes].bitcast(I32)
+            out=w_words[:, :query_bytes].bitcast(I32),
+            in_=wqkv_words[0, :, :query_bytes].bitcast(I32),
         )
 
         eps = sbuf.tile([P, 1], F32)
@@ -67,16 +68,17 @@ def tile_attention_pa_s_kernel(
                 out=w_scales[r:P:32, :].bitcast(I32),
                 in_=wqkv_scales[0, r:16:4, :].bitcast(I32),
             )
-        k_gain = sbuf.tile([P, HEAD], BF16)
-        nc.sync.dma_start(out=k_gain[:], in_=k_norm_w.partition_broadcast(P))
+        key_gain = sbuf.tile([P, HEAD], BF16)
+        nc.sync.dma_start(out=key_gain[:], in_=k_norm_w.partition_broadcast(P))
         nc.sync.dma_start(
-            out=w_words[:, q_bytes:].bitcast(I32), in_=wqkv_words[0, :, q_bytes:].bitcast(I32)
+            out=w_words[:, query_bytes:].bitcast(I32),
+            in_=wqkv_words[0, :, query_bytes:].bitcast(I32),
         )
 
         fc_sb = sbuf.tile([P, PAIRS, 2], BF16)
         nc.scalar.dma_start(out=fc_sb[:].rearrange("p j e -> p (j e)"), in_=fc_rows)
-        q_gain = sbuf.tile([P, HEAD], BF16)
-        nc.scalar.dma_start(out=q_gain[:], in_=q_norm_w.partition_broadcast(P))
+        query_gain = sbuf.tile([P, HEAD], BF16)
+        nc.scalar.dma_start(out=query_gain[:], in_=q_norm_w.partition_broadcast(P))
         warm = sbuf.tile([P, 1], F32)
         nc.scalar.activation(out=warm[:], in_=eps[:], func=ACT.Abs_reciprocal_sqrt)
 
@@ -86,7 +88,7 @@ def tile_attention_pa_s_kernel(
         x_words = x_sb[:].bitcast(F32)
         xt = psum.tile([P, 2, P], F32)
         for u in range(2):
-            nc.tensor.transpose(xt[:, u, :], x_words[:, u : K // 2 : 2], ident[:])
+            nc.tensor.transpose(xt[:, u, :], x_words[:, u : DIM // 2 : 2], ident[:])
         x_grouped = sbuf.tile([P, 4 * P], BF16, align_bytes=64)
         nc.scalar.copy(
             out=x_grouped[:].bitcast(F32).rearrange("p (r u) -> p r u", u=2),
@@ -100,20 +102,19 @@ def tile_attention_pa_s_kernel(
 
         first_head = [sum(PASS_HEADS[:i]) for i in range(len(PASS_HEADS))]
         sums = []
-        for head0, n in zip(first_head, PASS_HEADS):
-            acc = psum.tile([P, n, HEAD], F32, name="acc%d" % head0)
+        for head0, n_heads in zip(first_head, PASS_HEADS):
+            acc = psum.tile([P, n_heads, HEAD], F32, name="acc%d" % head0)
             nc.tensor.matmul_mx(
                 out=acc[:].rearrange("p n c -> p (n c)"),
                 lhsT=x_codes[:].bitcast(FP8X4),
                 lhsT_scale=x_scales[:],
-                rhs=w_words[:, 2 * HEAD * head0 : 2 * HEAD * (head0 + n)].bitcast(FP4X4),
-                rhs_scale=w_scales[:, HEAD * head0 : HEAD * (head0 + n)],
+                rhs=w_words[:, 2 * HEAD * head0 : 2 * HEAD * (head0 + n_heads)].bitcast(FP4X4),
+                rhs_scale=w_scales[:, HEAD * head0 : HEAD * (head0 + n_heads)],
                 start=True,
                 stop=True,
             )
             sums.append(acc)
-        head_sums = [acc[:, i, :] for acc, n in zip(sums, PASS_HEADS) for i in range(n)]
-        v_sums = sums[K_PASS + 1]
+        head_sums = [s[:, m, :] for s, n_heads in zip(sums, PASS_HEADS) for m in range(n_heads)]
 
         rot = sbuf.tile([P, PAIRS, 2, 2], BF16)
         nc.vector.tensor_copy(out=rot[:, :, 0, :], in_=fc_sb[:])
@@ -130,15 +131,15 @@ def tile_attention_pa_s_kernel(
             )
             return table
 
-        q_table = rotation_table(nc.vector, q_gain, "q_table")
-        k_table = rotation_table(nc.gpsimd, k_gain, "k_table")
+        query_table = rotation_table(nc.vector, query_gain, "query_table")
+        key_table = rotation_table(nc.gpsimd, key_gain, "key_table")
 
         squares = sbuf.tile([P, NORMED_HEADS, HEAD], F32)
         sumsq = sbuf.tile([P, NORMED_HEADS], F32)
         rstd = sbuf.tile([P, NORMED_HEADS], F32)
 
-        def inverse_rms(g):
-            heads = slice(GROUP * g, GROUP * (g + 1))
+        def inverse_rms(head0):
+            heads = slice(head0, head0 + GROUP)
             nc.scalar.activation(
                 out=rstd[:, heads], in_=sumsq[:, heads], func=ACT.Abs_reciprocal_sqrt,
                 scale=1.0 / HEAD, bias=eps[:],
@@ -150,10 +151,10 @@ def tile_attention_pa_s_kernel(
                 accum_out=sumsq[:, h : h + 1],
             )
             if h % GROUP == 0 and h > 0:
-                inverse_rms(h // GROUP - 1)
-        inverse_rms(N_GROUPS - 1)
-        v_sb = sbuf.tile([P, V_HEADS * HEAD], F32)
-        nc.scalar.copy(out=v_sb[:], in_=v_sums[:].rearrange("p n c -> p (n c)"))
+                inverse_rms(h - GROUP)
+        inverse_rms(NORMED_HEADS - GROUP)
+        value_sb = sbuf.tile([P, VALUE_HEADS * HEAD], F32)
+        nc.scalar.copy(out=value_sb[:], in_=sums[VALUE_PASS][:].rearrange("p n c -> p (n c)"))
 
         def products(i, table):
             prod = sbuf.tile([P, PASS_HEADS[i], HEAD, 2], F32, name="prod%d" % i)
@@ -169,25 +170,31 @@ def tile_attention_pa_s_kernel(
                 )
             return prod
 
-        def add_and_store(engine, prod, m0, m1, dest, name):
+        def add_and_store(engine, prod, m0, m1, dest, dest_head0, kind):
             pairs = prod[:, m0:m1, :, :].rearrange("p h (j a) e -> p (h j) a e", a=2)
-            rotated = sbuf.tile([P, (m1 - m0) * PAIRS, 2], F32, name=name)
+            rotated = sbuf.tile(
+                [P, (m1 - m0) * PAIRS, 2], F32, name="%s_rotated%d" % (kind, dest_head0 + m0)
+            )
             engine.tensor_tensor(
                 out=rotated[:], in0=pairs[:, :, 0, :], in1=pairs[:, :, 1, :], op=ALU.add
             )
-            nc.sync.dma_start(out=dest, in_=rotated[:].rearrange("p n e -> p (n e)"))
+            nc.sync.dma_start(
+                out=dest[:, :, HEAD * (dest_head0 + m0) : HEAD * (dest_head0 + m1)],
+                in_=rotated[:].rearrange("p n e -> p (n e)"),
+            )
 
-        for i in range(N_Q_PASSES):
-            n = PASS_HEADS[i]
-            prod = products(i, q_table)
-            add_and_store(
-                nc.gpsimd, prod, 0, n,
-                q_out[:, :, HEAD * first_head[i] : HEAD * (first_head[i] + n)], "q_rot%d" % i,
-            )
-            if i == N_Q_PASSES - 2:
-                nc.sync.dma_start(out=v_out, in_=v_sb[:])
-        prod = products(K_PASS, k_table)
-        for m0 in range(0, K_HEADS, GROUP):
-            add_and_store(
-                nc.vector, prod, m0, m0 + GROUP, k_out[:, :, HEAD * m0 : HEAD * (m0 + GROUP)], "k_rot%d" % m0
-            )
+        for i in range(LAST_QUERY_PASS):
+            prod = products(i, query_table)
+            add_and_store(nc.gpsimd, prod, 0, PASS_HEADS[i], query_out, first_head[i], "query")
+        nc.sync.dma_start(out=value_out, in_=value_sb[:])
+        n_last = PASS_HEADS[LAST_QUERY_PASS]
+        query_prod = products(LAST_QUERY_PASS, query_table)
+        add_and_store(
+            nc.gpsimd, query_prod, 0, n_last - GROUP, query_out, first_head[LAST_QUERY_PASS], "query"
+        )
+        key_prod = products(KEY_PASS, key_table)
+        add_and_store(
+            nc.vector, query_prod, n_last - GROUP, n_last, query_out, first_head[LAST_QUERY_PASS], "query"
+        )
+        for m0 in range(0, KEY_HEADS, GROUP):
+            add_and_store(nc.vector, key_prod, m0, m0 + GROUP, key_out, 0, "key")

@@ -59,6 +59,11 @@ def tile_attention_pa_s_kernel(
             in_=wqkv_words[0, :, :query_bytes].bitcast(I32),
         )
 
+        fc_sb = sbuf.tile([P, PAIRS, 2], BF16)
+        nc.sync.dma_start(out=fc_sb[:].rearrange("p j e -> p (j e)"), in_=fc_rows)
+        query_gain = sbuf.tile([P, HEAD], BF16)
+        nc.sync.dma_start(out=query_gain[:], in_=q_norm_w.partition_broadcast(P))
+
         eps = sbuf.tile([P, 1], F32)
         nc.vector.memset(eps[:], EPS)
         w_scales = sbuf.tile([P, COLS], U8, align_bytes=64)
@@ -75,10 +80,6 @@ def tile_attention_pa_s_kernel(
             in_=wqkv_words[0, :, query_bytes:].bitcast(I32),
         )
 
-        fc_sb = sbuf.tile([P, PAIRS, 2], BF16)
-        nc.scalar.dma_start(out=fc_sb[:].rearrange("p j e -> p (j e)"), in_=fc_rows)
-        query_gain = sbuf.tile([P, HEAD], BF16)
-        nc.scalar.dma_start(out=query_gain[:], in_=q_norm_w.partition_broadcast(P))
         warm = sbuf.tile([P, 1], F32)
         nc.scalar.activation(out=warm[:], in_=eps[:], func=ACT.Abs_reciprocal_sqrt)
 

@@ -95,6 +95,10 @@ def tile_attention_pa_s_kernel(
             out=x_grouped[:].bitcast(F32).rearrange("p (r u) -> p r u", u=2),
             in_=xt[:].rearrange("p u r -> p r u"),
         )
+        rot = sbuf.tile([P, PAIRS, 2, 2], BF16)
+        nc.vector.tensor_copy(out=rot[:, :, 0, :], in_=fc_sb[:])
+        nc.vector.tensor_copy(out=rot[:, :, 1, 1:2], in_=fc_sb[:, :, 0:1])
+        nc.vector.tensor_scalar_mul(out=rot[:, :, 1, 0:1], in0=fc_sb[:, :, 1:2], scalar1=-1.0)
         x_codes = sbuf.tile([P, P], U32, align_bytes=64)
         x_scales = sbuf.tile([P, P], U8, align_bytes=64)
         nc.vector.quantize_mx(
@@ -117,10 +121,6 @@ def tile_attention_pa_s_kernel(
             sums.append(acc)
         head_sums = [s[:, m, :] for s, n_heads in zip(sums, PASS_HEADS) for m in range(n_heads)]
 
-        rot = sbuf.tile([P, PAIRS, 2, 2], BF16)
-        nc.vector.tensor_copy(out=rot[:, :, 0, :], in_=fc_sb[:])
-        nc.vector.tensor_copy(out=rot[:, :, 1, 1:2], in_=fc_sb[:, :, 0:1])
-        nc.vector.tensor_scalar_mul(out=rot[:, :, 1, 0:1], in0=fc_sb[:, :, 1:2], scalar1=-1.0)
 
         def rotation_table(engine, gain, name):
             table = sbuf.tile([P, HEAD, 2], F32, name=name)

@@ -24,10 +24,8 @@ KEY_HEADS = 4
 VALUE_HEADS = 4
 NORMED_HEADS = QUERY_HEADS + KEY_HEADS
 COLS = (NORMED_HEADS + VALUE_HEADS) * HEAD
-PASS_HEADS = (2, 2, 4, 4, 4, 4, 4)
-LAST_QUERY_PASS = 4
-KEY_PASS = 5
-VALUE_PASS = 6
+PASS_HEADS = (2, 2, 2, 2, 4, 4, 4, 4)
+VALUE_PASS = 7
 GROUP = 2
 EPS = 1e-6
 
@@ -87,13 +85,14 @@ def tile_attention_pa_s_kernel(
         make_identity(nc, ident[:])
 
         x_words = x_sb[:].bitcast(F32)
-        xt = psum.tile([P, 2, P], F32)
+        value_acc = psum.tile([P, VALUE_HEADS, HEAD], F32)
+        xt = value_acc[:, 0:2, :]
         for u in range(2):
             nc.tensor.transpose(xt[:, u, :], x_words[:, u : DIM // 2 : 2], ident[:])
         x_grouped = sbuf.tile([P, 4 * P], BF16, align_bytes=64)
         nc.scalar.copy(
             out=x_grouped[:].bitcast(F32).rearrange("p (r u) -> p r u", u=2),
-            in_=xt[:].rearrange("p u r -> p r u"),
+            in_=xt.rearrange("p u r -> p r u"),
         )
         rot = sbuf.tile([P, PAIRS, 2, 2], BF16)
         nc.vector.tensor_copy(out=rot[:, :, 0, :], in_=fc_sb[:])
@@ -108,7 +107,10 @@ def tile_attention_pa_s_kernel(
         first_head = [sum(PASS_HEADS[:i]) for i in range(len(PASS_HEADS))]
         sums = []
         for head0, n_heads in zip(first_head, PASS_HEADS):
-            acc = psum.tile([P, n_heads, HEAD], F32, name="acc%d" % head0)
+            if head0 == NORMED_HEADS:
+                acc = value_acc
+            else:
+                acc = psum.tile([P, n_heads, HEAD], F32, name="acc%d" % head0)
             nc.tensor.matmul_mx(
                 out=acc[:].rearrange("p n c -> p (n c)"),
                 lhsT=x_codes[:].bitcast(FP8X4),
@@ -157,12 +159,12 @@ def tile_attention_pa_s_kernel(
         value_sb = sbuf.tile([P, VALUE_HEADS * HEAD], F32)
         nc.scalar.copy(out=value_sb[:], in_=sums[VALUE_PASS][:].rearrange("p n c -> p (n c)"))
 
-        def products(i, table):
-            prod = sbuf.tile([P, PASS_HEADS[i], HEAD, 2], F32, name="prod%d" % i)
-            for m in range(PASS_HEADS[i]):
-                h = first_head[i] + m
+        def products(head0, head1):
+            table = query_table if head0 < QUERY_HEADS else key_table
+            prod = sbuf.tile([P, head1 - head0, HEAD, 2], F32, name="prod%d" % head0)
+            for h in range(head0, head1):
                 nc.vector.scalar_tensor_tensor(
-                    out=prod[:, m, :, :],
+                    out=prod[:, h - head0, :, :],
                     in0=head_sums[h].unsqueeze(2).to_broadcast([P, HEAD, 2]),
                     scalar=rstd[:, h : h + 1],
                     in1=table[:],
@@ -171,31 +173,28 @@ def tile_attention_pa_s_kernel(
                 )
             return prod
 
-        def add_and_store(engine, prod, m0, m1, dest, dest_head0, kind):
-            pairs = prod[:, m0:m1, :, :].rearrange("p h (j a) e -> p (h j) a e", a=2)
-            rotated = sbuf.tile(
-                [P, (m1 - m0) * PAIRS, 2], F32, name="%s_rotated%d" % (kind, dest_head0 + m0)
-            )
+        def add_and_store(engine, prod, head0, head1):
+            pairs = prod[:].rearrange("p h (j a) e -> p (h j) a e", a=2)
+            rotated = sbuf.tile([P, (head1 - head0) * PAIRS, 2], F32, name="rotated%d" % head0)
             engine.tensor_tensor(
                 out=rotated[:], in0=pairs[:, :, 0, :], in1=pairs[:, :, 1, :], op=ALU.add
             )
+            dest = query_out if head0 < QUERY_HEADS else key_out
+            first = head0 if head0 < QUERY_HEADS else head0 - QUERY_HEADS
             nc.sync.dma_start(
-                out=dest[:, :, HEAD * (dest_head0 + m0) : HEAD * (dest_head0 + m1)],
+                out=dest[:, :, HEAD * first : HEAD * (first + head1 - head0)],
                 in_=rotated[:].rearrange("p n e -> p (n e)"),
             )
 
-        for i in range(LAST_QUERY_PASS):
-            prod = products(i, query_table)
-            add_and_store(nc.gpsimd, prod, 0, PASS_HEADS[i], query_out, first_head[i], "query")
+        for head0, head1 in ((0, 2), (2, 4), (4, 8), (8, 12)):
+            add_and_store(nc.gpsimd, products(head0, head1), head0, head1)
         nc.sync.dma_start(out=value_out, in_=value_sb[:])
-        n_last = PASS_HEADS[LAST_QUERY_PASS]
-        query_prod = products(LAST_QUERY_PASS, query_table)
-        add_and_store(
-            nc.gpsimd, query_prod, 0, n_last - GROUP, query_out, first_head[LAST_QUERY_PASS], "query"
-        )
-        key_prod = products(KEY_PASS, key_table)
-        add_and_store(
-            nc.vector, query_prod, n_last - GROUP, n_last, query_out, first_head[LAST_QUERY_PASS], "query"
-        )
-        for m0 in range(0, KEY_HEADS, GROUP):
-            add_and_store(nc.vector, key_prod, m0, m0 + GROUP, key_out, 0, "key")
+        gpsimd_last = products(12, 14)
+        vector_groups = [(14, 16)]
+        vector_prods = [products(14, 16)]
+        add_and_store(nc.gpsimd, gpsimd_last, 12, 14)
+        for head0 in range(QUERY_HEADS, NORMED_HEADS, GROUP):
+            vector_groups.append((head0, head0 + GROUP))
+            vector_prods.append(products(head0, head0 + GROUP))
+        for prod, (head0, head1) in zip(vector_prods, vector_groups):
+            add_and_store(nc.vector, prod, head0, head1)

@@ -57,13 +57,16 @@ def tile_attention_pa_s_kernel(
             in_=wqkv_words[0, :, :query_bytes].bitcast(I32),
         )
 
-        fc_sb = sbuf.tile([P, PAIRS, 2], BF16)
-        nc.sync.dma_start(out=fc_sb[:].rearrange("p j e -> p (j e)"), in_=fc_rows)
+        rot = sbuf.tile([P, 2, PAIRS, 2], BF16)
+        nc.sync.dma_start(out=rot[:, 0, :, :].rearrange("p j e -> p (j e)"), in_=fc_rows)
         query_gain = sbuf.tile([P, HEAD], BF16)
         nc.sync.dma_start(out=query_gain[:], in_=q_norm_w.partition_broadcast(P))
 
         eps = sbuf.tile([P, 1], F32)
         nc.vector.memset(eps[:], EPS)
+        sign = sbuf.tile([P, 2], BF16)
+        nc.vector.memset(sign[:, 0:1], -1.0)
+        nc.vector.memset(sign[:, 1:2], 1.0)
         w_scales = sbuf.tile([P, COLS], U8, align_bytes=64)
         nc.vector.memset(w_scales[:].bitcast(I32), 0)
         for r in range(4):
@@ -94,10 +97,12 @@ def tile_attention_pa_s_kernel(
             out=x_grouped[:].bitcast(F32).rearrange("p (r u) -> p r u", u=2),
             in_=xt.rearrange("p u r -> p r u"),
         )
-        rot = sbuf.tile([P, PAIRS, 2, 2], BF16)
-        nc.vector.tensor_copy(out=rot[:, :, 0, :], in_=fc_sb[:])
-        nc.vector.tensor_copy(out=rot[:, :, 1, 1:2], in_=fc_sb[:, :, 0:1])
-        nc.vector.tensor_scalar_mul(out=rot[:, :, 1, 0:1], in0=fc_sb[:, :, 1:2], scalar1=-1.0)
+        nc.vector.tensor_tensor(
+            out=rot[:, 1, :, :],
+            in0=rot[:, 0, :, ::-1],
+            in1=sign[:].unsqueeze(1).to_broadcast([P, PAIRS, 2]),
+            op=ALU.mult,
+        )
         x_codes = sbuf.tile([P, P], U32, align_bytes=64)
         x_scales = sbuf.tile([P, P], U8, align_bytes=64)
         nc.vector.quantize_mx(
@@ -127,9 +132,12 @@ def tile_attention_pa_s_kernel(
         def rotation_table(engine, gain, name):
             table = sbuf.tile([P, HEAD, 2], F32, name=name)
             engine.tensor_tensor(
-                out=table[:],
-                in0=rot[:].rearrange("p j a e -> p (j a) e"),
-                in1=gain[:].unsqueeze(2).to_broadcast([P, HEAD, 2]),
+                out=table[:].rearrange("p (j a) e -> p j a e", a=2),
+                in0=rot[:].rearrange("p a j e -> p j a e"),
+                in1=gain[:]
+                .rearrange("p (j a) -> p j a", a=2)
+                .unsqueeze(3)
+                .to_broadcast([P, PAIRS, 2, 2]),
                 op=ALU.mult,
             )
             return table

@@ -24,9 +24,9 @@ KEY_HEADS = 4
 VALUE_HEADS = 4
 NORMED_HEADS = QUERY_HEADS + KEY_HEADS
 COLS = (NORMED_HEADS + VALUE_HEADS) * HEAD
-PASS_HEADS = (2, 2, 2, 2, 4, 4, 4, 4)
-VALUE_PASS = 7
+PASSES = ((0, 2), (4, 2), (2, 2), (6, 2), (8, 4), (12, 4), (16, 4), (20, 4))
 GROUP = 2
+EARLY_HEADS = 4
 EPS = 1e-6
 
 FLOPS = 2 * P * DIM * COLS
@@ -109,15 +109,16 @@ def tile_attention_pa_s_kernel(
             out=x_codes[:].bitcast(FP8X4), scales=x_scales[:], in_=x_grouped[:]
         )
 
-        first_head = [sum(PASS_HEADS[:i]) for i in range(len(PASS_HEADS))]
-        sums = []
-        for head0, n_heads in zip(first_head, PASS_HEADS):
+        sums = {}
+        head_sums = {}
+        for head0, n_heads in PASSES:
             if head0 == NORMED_HEADS:
                 acc = value_acc
             else:
-                acc = psum.tile([P, n_heads, HEAD], F32, name="acc%d" % head0)
+                width = EARLY_HEADS if head0 == EARLY_HEADS else n_heads
+                acc = psum.tile([P, width, HEAD], F32, name="acc%d" % head0)
             nc.tensor.matmul_mx(
-                out=acc[:].rearrange("p n c -> p (n c)"),
+                out=acc[:, :n_heads, :].rearrange("p n c -> p (n c)"),
                 lhsT=x_codes[:].bitcast(FP8X4),
                 lhsT_scale=x_scales[:],
                 rhs=w_words[:, 2 * HEAD * head0 : 2 * HEAD * (head0 + n_heads)].bitcast(FP4X4),
@@ -125,8 +126,9 @@ def tile_attention_pa_s_kernel(
                 start=True,
                 stop=True,
             )
-            sums.append(acc)
-        head_sums = [s[:, m, :] for s, n_heads in zip(sums, PASS_HEADS) for m in range(n_heads)]
+            sums[head0] = acc
+            for m in range(n_heads):
+                head_sums[head0 + m] = acc[:, m, :]
 
 
         def rotation_table(engine, gain, name):
@@ -145,6 +147,18 @@ def tile_attention_pa_s_kernel(
         query_table = rotation_table(nc.vector, query_gain, "query_table")
         key_table = rotation_table(nc.gpsimd, key_gain, "key_table")
 
+        table_by_pair = query_table[:].rearrange("p (j a) e -> p j a e", a=2)
+        early = sbuf.tile([P, 2, EARLY_HEADS, PAIRS, 2], F32)
+        for head0 in range(0, EARLY_HEADS, GROUP):
+            by_pair = sums[head0][:].rearrange("p h (j a) -> p h j a", a=2)
+            for a in range(2):
+                nc.vector.tensor_tensor(
+                    out=early[:, a, head0 : head0 + GROUP, :, :],
+                    in0=by_pair[:, :, :, a : a + 1].to_broadcast([P, GROUP, PAIRS, 2]),
+                    in1=table_by_pair[:, :, a, :].unsqueeze(1).to_broadcast([P, GROUP, PAIRS, 2]),
+                    op=ALU.mult,
+                )
+
         squares = sbuf.tile([P, NORMED_HEADS, HEAD], F32)
         sumsq = sbuf.tile([P, NORMED_HEADS], F32)
         rstd = sbuf.tile([P, NORMED_HEADS], F32)
@@ -156,16 +170,31 @@ def tile_attention_pa_s_kernel(
                 scale=1.0 / HEAD, bias=eps[:],
             )
 
-        for h in range(NORMED_HEADS):
-            nc.scalar.activation(
-                out=squares[:, h, :], in_=head_sums[h], func=ACT.Square,
-                accum_out=sumsq[:, h : h + 1],
-            )
-            if h % GROUP == 0 and h > 0:
-                inverse_rms(h - GROUP)
-        inverse_rms(NORMED_HEADS - GROUP)
         value_sb = sbuf.tile([P, VALUE_HEADS * HEAD], F32)
-        nc.scalar.copy(out=value_sb[:], in_=sums[VALUE_PASS][:].rearrange("p n c -> p (n c)"))
+        square_order = [4, 6, 8, 10, 12, 14, 16, 18, 0, 2]
+        for i, head0 in enumerate(square_order):
+            if head0 == 0:
+                inverse_rms(square_order[i - 1])
+                nc.scalar.copy(
+                    out=value_sb[:], in_=value_acc[:].rearrange("p n c -> p (n c)")
+                )
+            for h in range(head0, head0 + GROUP):
+                nc.scalar.activation(
+                    out=squares[:, h, :], in_=head_sums[h], func=ACT.Square,
+                    accum_out=sumsq[:, h : h + 1],
+                )
+                if h == head0 and i > 1 and head0 != 0:
+                    inverse_rms(square_order[i - 1])
+            if i == 0:
+                inverse_rms(head0)
+        inverse_rms(square_order[-1])
+
+        def store(rotated, head0, head1):
+            dest = query_out if head0 < QUERY_HEADS else key_out
+            first = head0 if head0 < QUERY_HEADS else head0 - QUERY_HEADS
+            nc.sync.dma_start(
+                out=dest[:, :, HEAD * first : HEAD * (first + head1 - head0)], in_=rotated
+            )
 
         def products(head0, head1):
             table = query_table if head0 < QUERY_HEADS else key_table
@@ -187,22 +216,34 @@ def tile_attention_pa_s_kernel(
             engine.tensor_tensor(
                 out=rotated[:], in0=pairs[:, :, 0, :], in1=pairs[:, :, 1, :], op=ALU.add
             )
-            dest = query_out if head0 < QUERY_HEADS else key_out
-            first = head0 if head0 < QUERY_HEADS else head0 - QUERY_HEADS
-            nc.sync.dma_start(
-                out=dest[:, :, HEAD * first : HEAD * (first + head1 - head0)],
-                in_=rotated[:].rearrange("p n e -> p (n e)"),
+            store(rotated[:].rearrange("p n e -> p (n e)"), head0, head1)
+
+        add_and_store(nc.gpsimd, products(4, 6), 4, 6)
+
+        early_sums = sums[EARLY_HEADS]
+        for a in range(2):
+            nc.tensor.matmul(
+                early_sums[:].rearrange("p h c -> p (h c)"),
+                lhsT=ident[:],
+                rhs=early[:, a, :, :, :].rearrange("p h j e -> p (h j e)"),
+                start=(a == 0),
+                stop=(a == 1),
+            )
+        early_rotated = sbuf.tile([P, EARLY_HEADS, HEAD], F32)
+        for h in range(EARLY_HEADS):
+            nc.scalar.activation(
+                out=early_rotated[:, h, :], in_=early_sums[:, h, :], func=ACT.Copy,
+                scale=rstd[:, h : h + 1],
             )
 
-        for head0, head1 in ((0, 2), (2, 4), (4, 8), (8, 12)):
+
+        for head0, head1 in ((6, 8), (8, 12), (12, 14), (14, 16)):
+            if head0 == 14:
+                store(early_rotated[:].rearrange("p h c -> p (h c)"), 0, EARLY_HEADS)
             add_and_store(nc.gpsimd, products(head0, head1), head0, head1)
-        nc.sync.dma_start(out=value_out, in_=value_sb[:])
-        gpsimd_last = products(12, 14)
-        vector_groups = [(14, 16)]
-        vector_prods = [products(14, 16)]
-        add_and_store(nc.gpsimd, gpsimd_last, 12, 14)
-        for head0 in range(QUERY_HEADS, NORMED_HEADS, GROUP):
-            vector_groups.append((head0, head0 + GROUP))
-            vector_prods.append(products(head0, head0 + GROUP))
-        for prod, (head0, head1) in zip(vector_prods, vector_groups):
+            if head0 == 6:
+                nc.sync.dma_start(out=value_out, in_=value_sb[:])
+        last = ((16, 18), (18, 20))
+        last_prods = [products(head0, head1) for head0, head1 in last]
+        for prod, (head0, head1) in zip(last_prods, last):
             add_and_store(nc.vector, prod, head0, head1)

@@ -27,6 +27,7 @@ COLS = (NORMED_HEADS + VALUE_HEADS) * HEAD
 PASSES = ((0, 2), (4, 2), (2, 2), (6, 2), (8, 4), (12, 4), (16, 4), (20, 4))
 GROUP = 2
 EARLY_HEADS = 4
+FIRST_LOAD_HEADS = 8
 EPS = 1e-6
 
 FLOPS = 2 * P * DIM * COLS
@@ -51,11 +52,25 @@ def tile_attention_pa_s_kernel(
         nc.sync.dma_start(out=x_sb[:], in_=x_rows)
 
         w_words = sbuf.tile([P, 2 * COLS], U8, align_bytes=64)
-        query_bytes = 2 * QUERY_HEADS * HEAD
-        nc.sync.dma_start(
-            out=w_words[:, :query_bytes].bitcast(I32),
-            in_=wqkv_words[0, :, :query_bytes].bitcast(I32),
-        )
+        w_scales = sbuf.tile([P, COLS], U8, align_bytes=64)
+
+        def load_words(cols):
+            byte_cols = slice(2 * cols.start, 2 * cols.stop)
+            nc.sync.dma_start(
+                out=w_words[:, byte_cols].bitcast(I32), in_=wqkv_words[0, :, byte_cols].bitcast(I32)
+            )
+
+        def load_scales(cols):
+            for r in range(4):
+                nc.sync.dma_start(
+                    out=w_scales[r:P:32, cols].bitcast(I32),
+                    in_=wqkv_scales[0, r:16:4, cols].bitcast(I32),
+                )
+
+        first_cols = slice(0, FIRST_LOAD_HEADS * HEAD)
+        other_cols = slice(FIRST_LOAD_HEADS * HEAD, COLS)
+        load_words(first_cols)
+        load_scales(first_cols)
 
         rot = sbuf.tile([P, 2, PAIRS, 2], BF16)
         nc.sync.dma_start(out=rot[:, 0, :, :].rearrange("p j e -> p (j e)"), in_=fc_rows)
@@ -67,19 +82,10 @@ def tile_attention_pa_s_kernel(
         sign = sbuf.tile([P, 2], BF16)
         nc.vector.memset(sign[:, 0:1], -1.0)
         nc.vector.memset(sign[:, 1:2], 1.0)
-        w_scales = sbuf.tile([P, COLS], U8, align_bytes=64)
-        nc.vector.memset(w_scales[:].bitcast(I32), 0)
-        for r in range(4):
-            nc.sync.dma_start(
-                out=w_scales[r:P:32, :].bitcast(I32),
-                in_=wqkv_scales[0, r:16:4, :].bitcast(I32),
-            )
+        load_words(other_cols)
+        load_scales(other_cols)
         key_gain = sbuf.tile([P, HEAD], BF16)
         nc.sync.dma_start(out=key_gain[:], in_=k_norm_w.partition_broadcast(P))
-        nc.sync.dma_start(
-            out=w_words[:, query_bytes:].bitcast(I32),
-            in_=wqkv_words[0, :, query_bytes:].bitcast(I32),
-        )
 
         warm = sbuf.tile([P, 1], F32)
         nc.scalar.activation(out=warm[:], in_=eps[:], func=ACT.Abs_reciprocal_sqrt)
@@ -183,9 +189,9 @@ def tile_attention_pa_s_kernel(
                     out=squares[:, h, :], in_=head_sums[h], func=ACT.Square,
                     accum_out=sumsq[:, h : h + 1],
                 )
-                if h == head0 and i > 1 and head0 != 0:
+                if h == head0 and i > 2 and head0 != 0:
                     inverse_rms(square_order[i - 1])
-            if i == 0:
+            if i < 2:
                 inverse_rms(head0)
         inverse_rms(square_order[-1])
 

@@ -27,7 +27,7 @@ COLS = (NORMED_HEADS + VALUE_HEADS) * HEAD
 PASSES = ((0, 2), (4, 2), (2, 2), (6, 2), (8, 4), (12, 4), (16, 4), (20, 4))
 GROUP = 2
 EARLY_HEADS = 4
-FIRST_LOAD_HEADS = 8
+FIRST_LOAD_HEADS = 12
 EPS = 1e-6
 
 FLOPS = 2 * P * DIM * COLS
@@ -179,7 +179,7 @@ def tile_attention_pa_s_kernel(
         value_sb = sbuf.tile([P, VALUE_HEADS * HEAD], F32)
         square_order = [4, 6, 8, 10, 12, 14, 16, 18, 0, 2]
         for i, head0 in enumerate(square_order):
-            if head0 == 0:
+            if head0 == QUERY_HEADS:
                 inverse_rms(square_order[i - 1])
                 nc.scalar.copy(
                     out=value_sb[:], in_=value_acc[:].rearrange("p n c -> p (n c)")
@@ -189,7 +189,7 @@ def tile_attention_pa_s_kernel(
                     out=squares[:, h, :], in_=head_sums[h], func=ACT.Square,
                     accum_out=sumsq[:, h : h + 1],
                 )
-                if h == head0 and i > 2 and head0 != 0:
+                if h == head0 and i > 2 and head0 != QUERY_HEADS:
                     inverse_rms(square_order[i - 1])
             if i < 2:
                 inverse_rms(head0)
@@ -243,11 +243,11 @@ def tile_attention_pa_s_kernel(
             )
 
 
-        for head0, head1 in ((6, 8), (8, 12), (12, 14), (14, 16)):
+        for head0, head1 in ((6, 8), (8, 10), (10, 12), (12, 14), (14, 16)):
             if head0 == 14:
                 store(early_rotated[:].rearrange("p h c -> p (h c)"), 0, EARLY_HEADS)
             add_and_store(nc.gpsimd, products(head0, head1), head0, head1)
-            if head0 == 6:
+            if head0 == 8:
                 nc.sync.dma_start(out=value_out, in_=value_sb[:])
         last = ((16, 18), (18, 20))
         last_prods = [products(head0, head1) for head0, head1 in last]

@@ -24,9 +24,11 @@ KEY_HEADS = 4
 VALUE_HEADS = 4
 NORMED_HEADS = QUERY_HEADS + KEY_HEADS
 COLS = (NORMED_HEADS + VALUE_HEADS) * HEAD
-PASSES = ((0, 2), (4, 2), (2, 2), (6, 2), (8, 4), (12, 4), (16, 4), (20, 4))
+PASSES = ((0, 2), (4, 2), (2, 2), (6, 2), (8, 2), (10, 2), (12, 4), (16, 4))
 GROUP = 2
 EARLY_HEADS = 4
+VALUE_BANK = 4
+EARLY_BANK = 6
 FIRST_LOAD_HEADS = 12
 EPS = 1e-6
 
@@ -94,8 +96,8 @@ def tile_attention_pa_s_kernel(
         make_identity(nc, ident[:])
 
         x_words = x_sb[:].bitcast(F32)
-        value_acc = psum.tile([P, VALUE_HEADS, HEAD], F32)
-        xt = value_acc[:, 0:2, :]
+        key_acc = psum.tile([P, KEY_HEADS, HEAD], F32)
+        xt = key_acc[:, 0:2, :]
         for u in range(2):
             nc.tensor.transpose(xt[:, u, :], x_words[:, u : DIM // 2 : 2], ident[:])
         x_grouped = sbuf.tile([P, 4 * P], BF16, align_bytes=64)
@@ -103,26 +105,13 @@ def tile_attention_pa_s_kernel(
             out=x_grouped[:].bitcast(F32).rearrange("p (r u) -> p r u", u=2),
             in_=xt.rearrange("p u r -> p r u"),
         )
-        nc.vector.tensor_tensor(
-            out=rot[:, 1, :, :],
-            in0=rot[:, 0, :, ::-1],
-            in1=sign[:].unsqueeze(1).to_broadcast([P, PAIRS, 2]),
-            op=ALU.mult,
-        )
         x_codes = sbuf.tile([P, P], U32, align_bytes=64)
         x_scales = sbuf.tile([P, P], U8, align_bytes=64)
         nc.vector.quantize_mx(
             out=x_codes[:].bitcast(FP8X4), scales=x_scales[:], in_=x_grouped[:]
         )
 
-        sums = {}
-        head_sums = {}
-        for head0, n_heads in PASSES:
-            if head0 == NORMED_HEADS:
-                acc = value_acc
-            else:
-                width = EARLY_HEADS if head0 == EARLY_HEADS else n_heads
-                acc = psum.tile([P, width, HEAD], F32, name="acc%d" % head0)
+        def project(acc, head0, n_heads):
             nc.tensor.matmul_mx(
                 out=acc[:, :n_heads, :].rearrange("p n c -> p (n c)"),
                 lhsT=x_codes[:].bitcast(FP8X4),
@@ -132,10 +121,26 @@ def tile_attention_pa_s_kernel(
                 start=True,
                 stop=True,
             )
+
+        sums = {}
+        head_sums = {}
+        for head0, n_heads in PASSES:
+            if head0 == QUERY_HEADS:
+                acc = key_acc
+            else:
+                width = 4 if head0 in (VALUE_BANK, EARLY_BANK) else n_heads
+                acc = psum.tile([P, width, HEAD], F32, name="acc%d" % head0)
+            project(acc, head0, n_heads)
             sums[head0] = acc
             for m in range(n_heads):
                 head_sums[head0 + m] = acc[:, m, :]
 
+        nc.vector.tensor_tensor(
+            out=rot[:, 1, :, :],
+            in0=rot[:, 0, :, ::-1],
+            in1=sign[:].unsqueeze(1).to_broadcast([P, PAIRS, 2]),
+            op=ALU.mult,
+        )
 
         def rotation_table(engine, gain, name):
             table = sbuf.tile([P, HEAD, 2], F32, name=name)
@@ -176,24 +181,18 @@ def tile_attention_pa_s_kernel(
                 scale=1.0 / HEAD, bias=eps[:],
             )
 
-        value_sb = sbuf.tile([P, VALUE_HEADS * HEAD], F32)
-        square_order = [4, 6, 8, 10, 12, 14, 16, 18, 0, 2]
-        for i, head0 in enumerate(square_order):
-            if head0 == QUERY_HEADS:
-                inverse_rms(square_order[i - 1])
-                nc.scalar.copy(
-                    out=value_sb[:], in_=value_acc[:].rearrange("p n c -> p (n c)")
-                )
-            for h in range(head0, head0 + GROUP):
-                nc.scalar.activation(
-                    out=squares[:, h, :], in_=head_sums[h], func=ACT.Square,
-                    accum_out=sumsq[:, h : h + 1],
-                )
-                if h == head0 and i > 2 and head0 != QUERY_HEADS:
-                    inverse_rms(square_order[i - 1])
-            if i < 2:
-                inverse_rms(head0)
-        inverse_rms(square_order[-1])
+        def square_sums(groups, before=None):
+            for head0 in groups:
+                for h in range(head0, head0 + GROUP):
+                    nc.scalar.activation(
+                        out=squares[:, h, :], in_=head_sums[h], func=ACT.Square,
+                        accum_out=sumsq[:, h : h + 1],
+                    )
+                    if h == head0 and before is not None:
+                        inverse_rms(before)
+                before = head0
+
+        square_sums((4, 6, 8, 10, 12, 14))
 
         def store(rotated, head0, head1):
             dest = query_out if head0 < QUERY_HEADS else key_out
@@ -226,7 +225,17 @@ def tile_attention_pa_s_kernel(
 
         add_and_store(nc.gpsimd, products(4, 6), 4, 6)
 
-        early_sums = sums[EARLY_HEADS]
+        value_acc = sums[VALUE_BANK]
+        project(value_acc, NORMED_HEADS, VALUE_HEADS)
+        value_sb = sbuf.tile([P, VALUE_HEADS * HEAD], F32)
+        nc.scalar.copy(out=value_sb[:], in_=value_acc[:].rearrange("p n c -> p (n c)"))
+        inverse_rms(14)
+        square_sums((16, 18, 0, 2))
+        inverse_rms(2)
+
+        add_and_store(nc.gpsimd, products(6, 8), 6, 8)
+
+        early_sums = sums[EARLY_BANK]
         for a in range(2):
             nc.tensor.matmul(
                 early_sums[:].rearrange("p h c -> p (h c)"),
@@ -235,21 +244,24 @@ def tile_attention_pa_s_kernel(
                 start=(a == 0),
                 stop=(a == 1),
             )
-        early_rotated = sbuf.tile([P, EARLY_HEADS, HEAD], F32)
-        for h in range(EARLY_HEADS):
-            nc.scalar.activation(
-                out=early_rotated[:, h, :], in_=early_sums[:, h, :], func=ACT.Copy,
-                scale=rstd[:, h : h + 1],
-            )
+        early_rotated = []
+        for head0 in range(0, EARLY_HEADS, GROUP):
+            rotated = sbuf.tile([P, GROUP, HEAD], F32, name="rotated%d" % head0)
+            for m in range(GROUP):
+                nc.scalar.activation(
+                    out=rotated[:, m, :], in_=early_sums[:, head0 + m, :], func=ACT.Copy,
+                    scale=rstd[:, head0 + m : head0 + m + 1],
+                )
+            early_rotated.append(rotated)
 
-
-        for head0, head1 in ((6, 8), (8, 10), (10, 12), (12, 14), (14, 16)):
-            if head0 == 14:
-                store(early_rotated[:].rearrange("p h c -> p (h c)"), 0, EARLY_HEADS)
+        for head0, head1 in ((8, 10), (10, 12), (12, 14)):
             add_and_store(nc.gpsimd, products(head0, head1), head0, head1)
             if head0 == 8:
                 nc.sync.dma_start(out=value_out, in_=value_sb[:])
-        last = ((16, 18), (18, 20))
+            if head0 == 10:
+                store(early_rotated[0][:].rearrange("p h c -> p (h c)"), 0, GROUP)
+        store(early_rotated[1][:].rearrange("p h c -> p (h c)"), GROUP, EARLY_HEADS)
+        last = ((14, 16), (16, 18), (18, 20))
         last_prods = [products(head0, head1) for head0, head1 in last]
         for prod, (head0, head1) in zip(last_prods, last):
             add_and_store(nc.vector, prod, head0, head1)

@@ -228,9 +228,7 @@ def tile_attention_pa_s_kernel(
         value_acc = sums[VALUE_BANK]
         project(value_acc, NORMED_HEADS, VALUE_HEADS)
         value_sb = sbuf.tile([P, VALUE_HEADS * HEAD], F32)
-        nc.scalar.copy(out=value_sb[:], in_=value_acc[:].rearrange("p n c -> p (n c)"))
-        inverse_rms(14)
-        square_sums((16, 18, 0, 2))
+        square_sums((16, 18, 0, 2), 14)
         inverse_rms(2)
 
         add_and_store(nc.gpsimd, products(6, 8), 6, 8)
@@ -257,6 +255,9 @@ def tile_attention_pa_s_kernel(
         for head0, head1 in ((8, 10), (10, 12), (12, 14)):
             add_and_store(nc.gpsimd, products(head0, head1), head0, head1)
             if head0 == 8:
+                nc.vector.tensor_copy(
+                    out=value_sb[:], in_=value_acc[:].rearrange("p n c -> p (n c)")
+                )
                 nc.sync.dma_start(out=value_out, in_=value_sb[:])
             if head0 == 10:
                 store(early_rotated[0][:].rearrange("p h c -> p (h c)"), 0, GROUP)

from contextlib import ExitStack

import concourse.mybir as mybir
from concourse.masks import make_identity

F32 = mybir.dt.float32
BF16 = mybir.dt.bfloat16
I32 = mybir.dt.int32
U8 = mybir.dt.uint8
U32 = mybir.dt.uint32
FP8X4 = mybir.dt.float8_e4m3fn_x4
FP4X4 = mybir.dt.float4_e2m1fn_x4
ACT = mybir.ActivationFunctionType
ALU = mybir.AluOpType

P = 128
BATCH = 2
SEQ = 64
DIM = 512
HEAD = 128
PAIRS = HEAD // 2
QUERY_HEADS = 16
KEY_HEADS = 4
VALUE_HEADS = 4
NORMED_HEADS = QUERY_HEADS + KEY_HEADS
COLS = (NORMED_HEADS + VALUE_HEADS) * HEAD
PASSES = ((0, 2), (4, 2), (2, 2), (6, 2), (8, 2), (10, 2), (12, 4), (16, 4))
GROUP = 2
EARLY_HEADS = 4
VALUE_BANK = 4
EARLY_BANK = 6
FIRST_LOAD_HEADS = 12
EPS = 1e-6

FLOPS = 2 * P * DIM * COLS


def tile_attention_pa_s_kernel(
    tc, x, freqs_cis, wqkv_words, wqkv_scales, q_norm_w, k_norm_w, out_0, out_1, out_2
):
    nc = tc.nc
    x_rows = x.rearrange("b s k -> s b k")
    fc_rows = freqs_cis.rearrange("s j e -> s (j e)").unsqueeze(1).to_broadcast([SEQ, BATCH, HEAD])
    query_out = out_0.rearrange("b s h d -> s b (h d)")
    key_out = out_1.rearrange("b s h d -> s b (h d)")
    value_out = out_2.rearrange("b s h d -> s b (h d)")

    with ExitStack() as ctx:
        sbuf = ctx.enter_context(tc.tile_pool(name="sbuf", bufs=1))
        psum = ctx.enter_context(tc.psum_pool(name="psum", bufs=1))
        ctx.enter_context(tc.manual_schedule())

        x_sb = sbuf.tile([P, DIM], BF16)
        nc.sync.dma_start(out=x_sb[:], in_=x_rows)

        w_words = sbuf.tile([P, 2 * COLS], U8, align_bytes=64)
        w_scales = sbuf.tile([P, COLS], U8, align_bytes=64)

        def load_words(cols):
            byte_cols = slice(2 * cols.start, 2 * cols.stop)
            nc.sync.dma_start(
                out=w_words[:, byte_cols].bitcast(I32), in_=wqkv_words[0, :, byte_cols].bitcast(I32)
            )

        def load_scales(cols):
            for r in range(4):
                nc.sync.dma_start(
                    out=w_scales[r:P:32, cols].bitcast(I32),
                    in_=wqkv_scales[0, r:16:4, cols].bitcast(I32),
                )

        first_cols = slice(0, FIRST_LOAD_HEADS * HEAD)
        other_cols = slice(FIRST_LOAD_HEADS * HEAD, COLS)
        load_words(first_cols)
        load_scales(first_cols)

        rot = sbuf.tile([P, 2, PAIRS, 2], BF16)
        nc.sync.dma_start(out=rot[:, 0, :, :].rearrange("p j e -> p (j e)"), in_=fc_rows)
        query_gain = sbuf.tile([P, HEAD], BF16)
        nc.sync.dma_start(out=query_gain[:], in_=q_norm_w.partition_broadcast(P))

        eps = sbuf.tile([P, 1], F32)
        nc.vector.memset(eps[:], EPS)
        sign = sbuf.tile([P, 2], BF16)
        nc.vector.memset(sign[:, 0:1], -1.0)
        nc.vector.memset(sign[:, 1:2], 1.0)
        load_words(other_cols)
        load_scales(other_cols)
        key_gain = sbuf.tile([P, HEAD], BF16)
        nc.sync.dma_start(out=key_gain[:], in_=k_norm_w.partition_broadcast(P))

        warm = sbuf.tile([P, 1], F32)
        nc.scalar.activation(out=warm[:], in_=eps[:], func=ACT.Abs_reciprocal_sqrt)

        ident = sbuf.tile([P, P], F32)
        make_identity(nc, ident[:])

        x_words = x_sb[:].bitcast(F32)
        key_acc = psum.tile([P, KEY_HEADS, HEAD], F32)
        xt = key_acc[:, 0:2, :]
        for u in range(2):
            nc.tensor.transpose(xt[:, u, :], x_words[:, u : DIM // 2 : 2], ident[:])
        x_grouped = sbuf.tile([P, 4 * P], BF16, align_bytes=64)
        nc.scalar.copy(
            out=x_grouped[:].bitcast(F32).rearrange("p (r u) -> p r u", u=2),
            in_=xt.rearrange("p u r -> p r u"),
        )
        x_codes = sbuf.tile([P, P], U32, align_bytes=64)
        x_scales = sbuf.tile([P, P], U8, align_bytes=64)
        nc.vector.quantize_mx(
            out=x_codes[:].bitcast(FP8X4), scales=x_scales[:], in_=x_grouped[:]
        )

        def project(acc, head0, n_heads):
            nc.tensor.matmul_mx(
                out=acc[:, :n_heads, :].rearrange("p n c -> p (n c)"),
                lhsT=x_codes[:].bitcast(FP8X4),
                lhsT_scale=x_scales[:],
                rhs=w_words[:, 2 * HEAD * head0 : 2 * HEAD * (head0 + n_heads)].bitcast(FP4X4),
                rhs_scale=w_scales[:, HEAD * head0 : HEAD * (head0 + n_heads)],
                start=True,
                stop=True,
            )

        sums = {}
        head_sums = {}
        for head0, n_heads in PASSES:
            if head0 == QUERY_HEADS:
                acc = key_acc
            else:
                width = 4 if head0 in (VALUE_BANK, EARLY_BANK) else n_heads
                acc = psum.tile([P, width, HEAD], F32, name="acc%d" % head0)
            project(acc, head0, n_heads)
            sums[head0] = acc
            for m in range(n_heads):
                head_sums[head0 + m] = acc[:, m, :]

        nc.vector.tensor_tensor(
            out=rot[:, 1, :, :],
            in0=rot[:, 0, :, ::-1],
            in1=sign[:].unsqueeze(1).to_broadcast([P, PAIRS, 2]),
            op=ALU.mult,
        )

        def rotation_table(engine, gain, name):
            table = sbuf.tile([P, HEAD, 2], F32, name=name)
            engine.tensor_tensor(
                out=table[:].rearrange("p (j a) e -> p j a e", a=2),
                in0=rot[:].rearrange("p a j e -> p j a e"),
                in1=gain[:]
                .rearrange("p (j a) -> p j a", a=2)
                .unsqueeze(3)
                .to_broadcast([P, PAIRS, 2, 2]),
                op=ALU.mult,
            )
            return table

        query_table = rotation_table(nc.vector, query_gain, "query_table")
        key_table = rotation_table(nc.gpsimd, key_gain, "key_table")

        table_by_pair = query_table[:].rearrange("p (j a) e -> p j a e", a=2)
        early = sbuf.tile([P, 2, EARLY_HEADS, PAIRS, 2], F32)
        for head0 in range(0, EARLY_HEADS, GROUP):
            by_pair = sums[head0][:].rearrange("p h (j a) -> p h j a", a=2)
            for a in range(2):
                nc.vector.tensor_tensor(
                    out=early[:, a, head0 : head0 + GROUP, :, :],
                    in0=by_pair[:, :, :, a : a + 1].to_broadcast([P, GROUP, PAIRS, 2]),
                    in1=table_by_pair[:, :, a, :].unsqueeze(1).to_broadcast([P, GROUP, PAIRS, 2]),
                    op=ALU.mult,
                )

        squares = sbuf.tile([P, NORMED_HEADS, HEAD], F32)
        sumsq = sbuf.tile([P, NORMED_HEADS], F32)
        rstd = sbuf.tile([P, NORMED_HEADS], F32)

        def inverse_rms(head0):
            heads = slice(head0, head0 + GROUP)
            nc.scalar.activation(
                out=rstd[:, heads], in_=sumsq[:, heads], func=ACT.Abs_reciprocal_sqrt,
                scale=1.0 / HEAD, bias=eps[:],
            )

        def square_sums(groups, before=None):
            for head0 in groups:
                for h in range(head0, head0 + GROUP):
                    nc.scalar.activation(
                        out=squares[:, h, :], in_=head_sums[h], func=ACT.Square,
                        accum_out=sumsq[:, h : h + 1],
                    )
                    if h == head0 and before is not None:
                        inverse_rms(before)
                before = head0

        square_sums((4, 6, 8, 10, 12, 14))

        def store(rotated, head0, head1):
            dest = query_out if head0 < QUERY_HEADS else key_out
            first = head0 if head0 < QUERY_HEADS else head0 - QUERY_HEADS
            nc.sync.dma_start(
                out=dest[:, :, HEAD * first : HEAD * (first + head1 - head0)], in_=rotated
            )

        def products(head0, head1):
            table = query_table if head0 < QUERY_HEADS else key_table
            prod = sbuf.tile([P, head1 - head0, HEAD, 2], F32, name="prod%d" % head0)
            for h in range(head0, head1):
                nc.vector.scalar_tensor_tensor(
                    out=prod[:, h - head0, :, :],
                    in0=head_sums[h].unsqueeze(2).to_broadcast([P, HEAD, 2]),
                    scalar=rstd[:, h : h + 1],
                    in1=table[:],
                    op0=ALU.mult,
                    op1=ALU.mult,
                )
            return prod

        def add_and_store(engine, prod, head0, head1):
            pairs = prod[:].rearrange("p h (j a) e -> p (h j) a e", a=2)
            rotated = sbuf.tile([P, (head1 - head0) * PAIRS, 2], F32, name="rotated%d" % head0)
            engine.tensor_tensor(
                out=rotated[:], in0=pairs[:, :, 0, :], in1=pairs[:, :, 1, :], op=ALU.add
            )
            store(rotated[:].rearrange("p n e -> p (n e)"), head0, head1)

        add_and_store(nc.gpsimd, products(4, 6), 4, 6)

        value_acc = sums[VALUE_BANK]
        project(value_acc, NORMED_HEADS, VALUE_HEADS)
        value_sb = sbuf.tile([P, VALUE_HEADS * HEAD], F32)
        square_sums((16, 18, 0, 2), 14)
        inverse_rms(2)

        add_and_store(nc.gpsimd, products(6, 8), 6, 8)

        early_sums = sums[EARLY_BANK]
        for a in range(2):
            nc.tensor.matmul(
                early_sums[:].rearrange("p h c -> p (h c)"),
                lhsT=ident[:],
                rhs=early[:, a, :, :, :].rearrange("p h j e -> p (h j e)"),
                start=(a == 0),
                stop=(a == 1),
            )
        early_rotated = []
        for head0 in range(0, EARLY_HEADS, GROUP):
            rotated = sbuf.tile([P, GROUP, HEAD], F32, name="rotated%d" % head0)
            for m in range(GROUP):
                nc.scalar.activation(
                    out=rotated[:, m, :], in_=early_sums[:, head0 + m, :], func=ACT.Copy,
                    scale=rstd[:, head0 + m : head0 + m + 1],
                )
            early_rotated.append(rotated)

        for head0, head1 in ((8, 10), (10, 12), (12, 14)):
            add_and_store(nc.gpsimd, products(head0, head1), head0, head1)
            if head0 == 8:
                nc.vector.tensor_copy(
                    out=value_sb[:], in_=value_acc[:].rearrange("p n c -> p (n c)")
                )
                nc.sync.dma_start(out=value_out, in_=value_sb[:])
            if head0 == 10:
                store(early_rotated[0][:].rearrange("p h c -> p (h c)"), 0, GROUP)
        store(early_rotated[1][:].rearrange("p h c -> p (h c)"), GROUP, EARLY_HEADS)
        last = ((14, 16), (16, 18), (18, 20))
        last_prods = [products(head0, head1) for head0, head1 in last]
        for prod, (head0, head1) in zip(last_prods, last):
            add_and_store(nc.vector, prod, head0, head1)
